import numpy as np
import ml_dtypes


def mxq(x, axis, fmt="e4m3"):
    dtype, down = {"e4m3": (ml_dtypes.float8_e4m3fn, 7), "e5m2": (ml_dtypes.float8_e5m2, 14)}[fmt]
    v = np.moveaxis(np.asarray(x, np.float32).astype(ml_dtypes.bfloat16).astype(np.float64), axis, -1)
    blocks = v.reshape(v.shape[:-1] + (-1, 32))
    amax = np.abs(blocks).max(-1, keepdims=True)
    byte = np.maximum(np.where(amax > 0, np.frexp(amax)[1] - 1 + 127, 0) - down, 1)
    scale = np.exp2(byte - 127.0)
    codes = (blocks / scale).astype(np.float32).astype(dtype).astype(np.float64)
    return np.moveaxis((codes * scale).reshape(v.shape), -1, axis)


WIDE = False


def mx_kscale(k):
    if not WIDE:
        return np.ones(k)
    levels = np.array([10, -10, 5, -5, 0])
    a = np.random.permutation(np.resize(levels, k // 512 * 4)).reshape(k // 512, 4)
    idx = np.arange(k)
    return np.exp2(a[idx // 512, idx % 128 // 32])


BF16 = ml_dtypes.bfloat16


def bf(x):
    return np.asarray(x, np.float32).astype(BF16)


def f64(x):
    return np.asarray(x).astype(np.float64)


B, C, T, N, KS = 1, 128, 1, 2048, 4


def setup_inputs():
    u = mx_kscale(KS * C)[:C]
    w = np.random.standard_normal((KS, C, C)) * 0.8 / np.sqrt(KS * C)
    w[1:] = w[1:] / u[:, None]
    return {"x": bf(np.random.standard_normal((B, C, T, N))),
            "x1": bf(np.random.standard_normal((B, T, N, C)) * 0.9 * u),
            "x2": bf(np.random.standard_normal((B, T, N, C)) * 1.9 * u),
            "gso": bf(np.random.standard_normal((N, N)) * 0.9 / np.sqrt(N)),
            "weight": bf(w),
            "bias": bf(np.random.standard_normal(C) * 0.5)}


def reference(x, x1, x2, gso, weight, bias):
    x0 = f64(x).transpose(0, 2, 3, 1)
    x1 = f64(x1)
    x2 = f64(x2)
    x3 = 2.0 * (mxq(f64(gso), 1, "e4m3") @ mxq(x2, 2, "e4m3")) - x1
    xs = np.concatenate([x0, x1, x2, x3], axis=3)
    cheb = (mxq(xs, 3, "e4m3") @ mxq(f64(weight).reshape(KS * C, C), 0, "e4m3")) + f64(bias)
    return cheb.transpose(0, 3, 1, 2) + f64(x)

@@ -1,0 +1,203 @@
+from contextlib import ExitStack
+
+import concourse.mybir as mybir
+from concourse.masks import make_identity
+
+BF16 = mybir.dt.bfloat16
+F32 = mybir.dt.float32
+U32 = mybir.dt.uint32
+U8 = mybir.dt.uint8
+FP8X4 = mybir.dt.float8_e4m3fn_x4
+MULT = mybir.AluOpType.mult
+ADD = mybir.AluOpType.add
+SUBTRACT = mybir.AluOpType.subtract
+
+P = 128
+PACK = 4
+NODES = 2048
+CH = 128
+ORDERS = 4
+K2 = ORDERS * CH
+PASSES = NODES // (P * PACK)
+PAIR = 2
+CHUNK = P * PAIR
+CHUNKS = NODES // CHUNK
+
+FLOPS = 2 * NODES * NODES * CH + 2 * NODES * K2 * CH
+
+
+def tile_graphconvlayer_pb_kernel(tc, x, x1, x2, gso, weight, bias, out):
+    nc = tc.nc
+    x_cn = x[0, :, 0, :]
+    out_cn = out[0, :, 0, :]
+    x1_split = x1[0, 0, :, :].rearrange("(a p e) c -> e p a c", p=P, e=PAIR)
+    x2_split = x2[0, 0, :, :].rearrange("(a p e) c -> e p a c", p=P, e=PAIR)
+    gso_split = gso.rearrange("(a p e) m -> a p e m", p=P, e=PAIR)
+
+    with ExitStack() as ctx:
+        keep = ctx.enter_context(tc.tile_pool(name="keep", bufs=1))
+        rows = ctx.enter_context(tc.tile_pool(name="rows", bufs=CHUNKS))
+        work = ctx.enter_context(tc.tile_pool(name="work", bufs=3))
+        psum_gso = ctx.enter_context(tc.psum_pool(name="psum_gso", bufs=4))
+        psum_one = ctx.enter_context(tc.psum_pool(name="psum_one", bufs=1))
+
+        ident = keep.tile([P, P], F32)
+        make_identity(nc, ident[:])
+
+        xs = keep.tile([P, CHUNKS, PAIR, K2], BF16)
+        x_sb = keep.tile([P, NODES], BF16)
+        w_raw = keep.tile([P, PACK, CH], BF16)
+        bias_bf = keep.tile([P, 1], BF16)
+        gso_rows = []
+        for a in range(CHUNKS):
+            gso_chunk = rows.tile([P, PAIR, NODES], BF16, name="gso_chunk")
+            gso_rows.append(gso_chunk)
+
+        nc.scalar.dma_start(
+            out=w_raw[:], in_=weight.rearrange("o i j -> (o i) j").rearrange("(p t) j -> p t j", t=PACK)
+        )
+        nc.scalar.dma_start(out=bias_bf[:], in_=bias.rearrange("(c o) -> c o", o=1))
+
+        nc.sync.dma_start(out=gso_rows[0][:], in_=gso_split[0])
+        for e in range(PAIR):
+            nc.sync.dma_start(out=xs[:, :, e, 2 * CH : 3 * CH], in_=x2_split[e])
+        nc.sync.dma_start(out=gso_rows[1][:], in_=gso_split[1])
+        nc.sync.dma_start(out=x_sb[:], in_=x_cn)
+        for e in range(PAIR):
+            nc.sync.dma_start(out=xs[:, :, e, CH : 2 * CH], in_=x1_split[e])
+        for a in range(2, CHUNKS):
+            nc.sync.dma_start(out=gso_rows[a][:], in_=gso_split[a])
+
+        bias_f32 = keep.tile([P, 1], F32)
+        nc.vector.tensor_copy(out=bias_f32[:], in_=bias_bf[:])
+
+        w_grouped = keep.tile([P, CH, PACK], BF16, align_bytes=64)
+        w_codes = keep.tile([P, CH], U32, align_bytes=64)
+        w_scales = keep.tile([P, CH], U8, align_bytes=64)
+        nc.vector.tensor_copy(out=w_grouped[:], in_=w_raw[:].rearrange("p t j -> p j t"))
+        nc.vector.quantize_mx(
+            out=w_codes[:].bitcast(FP8X4), scales=w_scales[:], in_=w_grouped[:].rearrange("p j t -> p (j t)")
+        )
+
+        x2_grouped = keep.tile([P, PASSES, CH, PACK], BF16, align_bytes=64)
+        x2_codes = keep.tile([P, PASSES, CH], U32, align_bytes=64)
+        x2_scales = keep.tile([P, PASSES, CH], U8, align_bytes=64)
+        for g in range(PASSES):
+            nc.vector.tensor_copy(
+                out=x2_grouped[:, g].rearrange("p c (u e) -> p c u e", e=PAIR),
+                in_=xs[:, 2 * g : 2 * g + 2, :, 2 * CH : 3 * CH].rearrange("p u e c -> p c u e"),
+            )
+        nc.vector.quantize_mx(
+            out=x2_codes[:].rearrange("p g c -> p (g c)").bitcast(FP8X4),
+            scales=x2_scales[:].rearrange("p g c -> p (g c)"),
+            in_=x2_grouped[:].rearrange("p g c t -> p (g c t)"),
+        )
+
+        x_words = x_sb[:].bitcast(F32)
+        xs_words = xs[:].bitcast(F32)
+        gso_codes = {}
+        gso_scales = {}
+        xs_codes = {}
+        xs_scales = {}
+
+        def transpose_gso(a):
+            words = gso_rows[a][:].bitcast(F32)
+            for e in range(PAIR):
+                grouped = work.tile([P, PASSES, P, PACK], BF16, name="gso_grouped", align_bytes=64)
+                grouped_words = grouped[:].bitcast(F32)
+                for half in range(PASSES // 2):
+                    bank = psum_gso.tile([P, 2, 2, P], F32, name="gso_bank")
+                    for g2 in range(2):
+                        for u in range(2):
+                            first = (4 * half + 2 * g2 + u) * P
+                            nc.tensor.transpose(bank[:, g2, u, :], words[:, e, first : first + P], ident[:])
+                    nc.scalar.copy(
+                        out=grouped_words[:, 2 * half : 2 * half + 2],
+                        in_=bank[:].rearrange("q g u n -> q g n u"),
+                    )
+                codes = work.tile([P, PASSES, P], U32, name="gso_codes", align_bytes=64, bufs=6)
+                scales = work.tile([P, PASSES, P], U8, name="gso_scales", align_bytes=64, bufs=6)
+                nc.vector.quantize_mx(
+                    out=codes[:].rearrange("q g n -> q (g n)").bitcast(FP8X4),
+                    scales=scales[:].rearrange("q g n -> q (g n)"),
+                    in_=grouped[:].rearrange("q g n t -> q (g n t)"),
+                )
+                gso_codes[(a, e)] = codes
+                gso_scales[(a, e)] = scales
+
+        def transpose_x(a):
+            bank = psum_one.tile([P, CH], F32, name="x_bank")
+            nc.tensor.transpose(bank[:], x_words[:, a * P : (a + 1) * P], ident[:])
+            nc.scalar.copy(
+                out=xs[:, a, :, 0:CH], in_=bank[:].bitcast(BF16).rearrange("p (c e) -> p e c", e=PAIR)
+            )
+
+        def first_matmul(a):
+            acc = psum_one.tile([P, PAIR, CH], F32, name="x3_acc")
+            for e in range(PAIR):
+                for g in range(PASSES):
+                    nc.tensor.matmul_mx(
+                        out=acc[:, e, :],
+                        lhsT=gso_codes[(a, e)][:, g, :].bitcast(FP8X4),
+                        lhsT_scale=gso_scales[(a, e)][:, g, :],
+                        rhs=x2_codes[:, g, :].bitcast(FP8X4),
+                        rhs_scale=x2_scales[:, g, :],
+                        start=(g == 0),
+                        stop=(g == PASSES - 1),
+                    )
+            nc.vector.scalar_tensor_tensor(
+                out=xs[:, a, :, 3 * CH : 4 * CH],
+                in0=acc[:],
+                scalar=2.0,
+                in1=xs[:, a, :, CH : 2 * CH],
+                op0=MULT,
+                op1=SUBTRACT,
+            )
+
+        def transpose_xs(a):
+            bank = psum_one.tile([P, PAIR, 2, P], F32, name="xs_bank")
+            for e in range(PAIR):
+                for u in range(2):
+                    nc.tensor.transpose(bank[:, e, u, :], xs_words[:, a, e, u : K2 // 2 : 2], ident[:])
+            grouped = work.tile([P, CHUNK, PACK], BF16, name="xs_grouped", align_bytes=64)
+            nc.scalar.copy(
+                out=grouped[:].bitcast(F32).rearrange("q (p e) u -> q p e u", e=PAIR),
+                in_=bank[:].rearrange("q e u p -> q p e u"),
+            )
+            codes = work.tile([P, CHUNK], U32, name="xs_codes", align_bytes=64)
+            scales = work.tile([P, CHUNK], U8, name="xs_scales", align_bytes=64)
+            nc.vector.quantize_mx(
+                out=codes[:].bitcast(FP8X4), scales=scales[:], in_=grouped[:].rearrange("q n t -> q (n t)")
+            )
+            xs_codes[a] = codes
+            xs_scales[a] = scales
+
+        def second_matmul(a):
+            acc = psum_one.tile([P, CHUNK], F32, name="out_acc")
+            nc.tensor.matmul_mx(
+                out=acc[:],
+                lhsT=w_codes[:].bitcast(FP8X4),
+                lhsT_scale=w_scales[:],
+                rhs=xs_codes[a][:].bitcast(FP8X4),
+                rhs_scale=xs_scales[a][:],
+                start=True,
+                stop=True,
+            )
+            nodes = slice(a * CHUNK, (a + 1) * CHUNK)
+            result = work.tile([P, CHUNK], F32, name="result")
+            nc.vector.scalar_tensor_tensor(
+                out=result[:], in0=acc[:], scalar=bias_f32[:, 0:1], in1=x_sb[:, nodes], op0=ADD, op1=ADD
+            )
+            nc.sync.dma_start(out=out_cn[:, nodes], in_=result[:])
+
+        for i in range(CHUNKS + 3):
+            if i < CHUNKS:
+                transpose_gso(i)
+            if 0 <= i - 1 < CHUNKS:
+                transpose_x(i - 1)
+            if 0 <= i - 2 < CHUNKS:
+                transpose_xs(i - 2)
+            if 0 <= i - 1 < CHUNKS:
+                first_matmul(i - 1)
+            if 0 <= i - 3 < CHUNKS:
+                second_matmul(i - 3)

@@ -32,7 +32,7 @@ def tile_graphconvlayer_pb_kernel(tc, x, x1, x2, gso, weight, bias, out):
     out_cn = out[0, :, 0, :]
     x1_split = x1[0, 0, :, :].rearrange("(a p e) c -> e p a c", p=P, e=PAIR)
     x2_split = x2[0, 0, :, :].rearrange("(a p e) c -> e p a c", p=P, e=PAIR)
-    gso_split = gso.rearrange("(a p e) m -> a p e m", p=P, e=PAIR)
+    gso_split = gso.rearrange("(a p e) m -> a e p m", p=P, e=PAIR)
 
     with ExitStack() as ctx:
         keep = ctx.enter_context(tc.tile_pool(name="keep", bufs=1))
@@ -40,6 +40,7 @@ def tile_graphconvlayer_pb_kernel(tc, x, x1, x2, gso, weight, bias, out):
         work = ctx.enter_context(tc.tile_pool(name="work", bufs=3))
         psum_gso = ctx.enter_context(tc.psum_pool(name="psum_gso", bufs=4))
         psum_one = ctx.enter_context(tc.psum_pool(name="psum_one", bufs=1))
+        ctx.enter_context(tc.manual_schedule())
 
         ident = keep.tile([P, P], F32)
         make_identity(nc, ident[:])
@@ -58,15 +59,19 @@ def tile_graphconvlayer_pb_kernel(tc, x, x1, x2, gso, weight, bias, out):
         )
         nc.scalar.dma_start(out=bias_bf[:], in_=bias.rearrange("(c o) -> c o", o=1))
 
-        nc.sync.dma_start(out=gso_rows[0][:], in_=gso_split[0])
+        def load_gso(a):
+            for e in range(PAIR):
+                nc.sync.dma_start(out=gso_rows[a][:, e, :], in_=gso_split[a, e])
+
+        load_gso(0)
         for e in range(PAIR):
             nc.sync.dma_start(out=xs[:, :, e, 2 * CH : 3 * CH], in_=x2_split[e])
-        nc.sync.dma_start(out=gso_rows[1][:], in_=gso_split[1])
+        load_gso(1)
         nc.sync.dma_start(out=x_sb[:], in_=x_cn)
         for e in range(PAIR):
             nc.sync.dma_start(out=xs[:, :, e, CH : 2 * CH], in_=x1_split[e])
         for a in range(2, CHUNKS):
-            nc.sync.dma_start(out=gso_rows[a][:], in_=gso_split[a])
+            load_gso(a)
 
         bias_f32 = keep.tile([P, 1], F32)
         nc.vector.tensor_copy(out=bias_f32[:], in_=bias_bf[:])
@@ -95,15 +100,19 @@ def tile_graphconvlayer_pb_kernel(tc, x, x1, x2, gso, weight, bias, out):
 
         x_words = x_sb[:].bitcast(F32)
         xs_words = xs[:].bitcast(F32)
+        gso_grouped = {}
         gso_codes = {}
         gso_scales = {}
+        x3_acc = {}
+        xs_grouped = {}
         xs_codes = {}
         xs_scales = {}
+        out_acc = {}
 
         def transpose_gso(a):
             words = gso_rows[a][:].bitcast(F32)
             for e in range(PAIR):
-                grouped = work.tile([P, PASSES, P, PACK], BF16, name="gso_grouped", align_bytes=64)
+                grouped = work.tile([P, PASSES, P, PACK], BF16, name="gso_grouped", align_bytes=64, bufs=4)
                 grouped_words = grouped[:].bitcast(F32)
                 for half in range(PASSES // 2):
                     bank = psum_gso.tile([P, 2, 2, P], F32, name="gso_bank")
@@ -111,16 +120,21 @@ def tile_graphconvlayer_pb_kernel(tc, x, x1, x2, gso, weight, bias, out):
                         for u in range(2):
                             first = (4 * half + 2 * g2 + u) * P
                             nc.tensor.transpose(bank[:, g2, u, :], words[:, e, first : first + P], ident[:])
-                    nc.scalar.copy(
+                    copy = nc.vector.tensor_copy if (e == PAIR - 1 and half == PASSES // 2 - 1) else nc.scalar.copy
+                    copy(
                         out=grouped_words[:, 2 * half : 2 * half + 2],
                         in_=bank[:].rearrange("q g u n -> q g n u"),
                     )
+                gso_grouped[(a, e)] = grouped
+
+        def quantise_gso(a):
+            for e in range(PAIR):
                 codes = work.tile([P, PASSES, P], U32, name="gso_codes", align_bytes=64, bufs=6)
                 scales = work.tile([P, PASSES, P], U8, name="gso_scales", align_bytes=64, bufs=6)
                 nc.vector.quantize_mx(
                     out=codes[:].rearrange("q g n -> q (g n)").bitcast(FP8X4),
                     scales=scales[:].rearrange("q g n -> q (g n)"),
-                    in_=grouped[:].rearrange("q g n t -> q (g n t)"),
+                    in_=gso_grouped[(a, e)][:].rearrange("q g n t -> q (g n t)"),
                 )
                 gso_codes[(a, e)] = codes
                 gso_scales[(a, e)] = scales
@@ -145,9 +159,12 @@ def tile_graphconvlayer_pb_kernel(tc, x, x1, x2, gso, weight, bias, out):
                         start=(g == 0),
                         stop=(g == PASSES - 1),
                     )
+            x3_acc[a] = acc
+
+        def finish_x3(a):
             nc.vector.scalar_tensor_tensor(
                 out=xs[:, a, :, 3 * CH : 4 * CH],
-                in0=acc[:],
+                in0=x3_acc[a][:],
                 scalar=2.0,
                 in1=xs[:, a, :, CH : 2 * CH],
                 op0=MULT,
@@ -164,10 +181,13 @@ def tile_graphconvlayer_pb_kernel(tc, x, x1, x2, gso, weight, bias, out):
                 out=grouped[:].bitcast(F32).rearrange("q (p e) u -> q p e u", e=PAIR),
                 in_=bank[:].rearrange("q e u p -> q p e u"),
             )
+            xs_grouped[a] = grouped
+
+        def quantise_xs(a):
             codes = work.tile([P, CHUNK], U32, name="xs_codes", align_bytes=64)
             scales = work.tile([P, CHUNK], U8, name="xs_scales", align_bytes=64)
             nc.vector.quantize_mx(
-                out=codes[:].bitcast(FP8X4), scales=scales[:], in_=grouped[:].rearrange("q n t -> q (n t)")
+                out=codes[:].bitcast(FP8X4), scales=scales[:], in_=xs_grouped[a][:].rearrange("q n t -> q (n t)")
             )
             xs_codes[a] = codes
             xs_scales[a] = scales
@@ -183,14 +203,25 @@ def tile_graphconvlayer_pb_kernel(tc, x, x1, x2, gso, weight, bias, out):
                 start=True,
                 stop=True,
             )
+            out_acc[a] = acc
+
+        def finish_out(a):
             nodes = slice(a * CHUNK, (a + 1) * CHUNK)
             result = work.tile([P, CHUNK], F32, name="result")
             nc.vector.scalar_tensor_tensor(
-                out=result[:], in0=acc[:], scalar=bias_f32[:, 0:1], in1=x_sb[:, nodes], op0=ADD, op1=ADD
+                out=result[:], in0=out_acc[a][:], scalar=bias_f32[:, 0:1], in1=x_sb[:, nodes], op0=ADD, op1=ADD
             )
             nc.sync.dma_start(out=out_cn[:, nodes], in_=result[:])
 
-        for i in range(CHUNKS + 3):
+        for i in range(CHUNKS + 4):
+            if 0 <= i - 2 < CHUNKS:
+                finish_x3(i - 2)
+            if 0 <= i - 1 < CHUNKS:
+                quantise_gso(i - 1)
+            if 0 <= i - 3 < CHUNKS:
+                quantise_xs(i - 3)
+            if 0 <= i - 4 < CHUNKS:
+                finish_out(i - 4)
             if i < CHUNKS:
                 transpose_gso(i)
             if 0 <= i - 1 < CHUNKS:

@@ -22,6 +22,7 @@ PASSES = NODES // (P * PACK)
 PAIR = 2
 CHUNK = P * PAIR
 CHUNKS = NODES // CHUNK
+TILES = NODES // P
 
 FLOPS = 2 * NODES * NODES * CH + 2 * NODES * K2 * CH
 
@@ -36,7 +37,7 @@ def tile_graphconvlayer_pb_kernel(tc, x, x1, x2, gso, weight, bias, out):
 
     with ExitStack() as ctx:
         keep = ctx.enter_context(tc.tile_pool(name="keep", bufs=1))
-        rows = ctx.enter_context(tc.tile_pool(name="rows", bufs=CHUNKS))
+        rows = ctx.enter_context(tc.tile_pool(name="rows", bufs=TILES))
         work = ctx.enter_context(tc.tile_pool(name="work", bufs=3))
         psum_gso = ctx.enter_context(tc.psum_pool(name="psum_gso", bufs=4))
         psum_one = ctx.enter_context(tc.psum_pool(name="psum_one", bufs=1))
@@ -50,28 +51,28 @@ def tile_graphconvlayer_pb_kernel(tc, x, x1, x2, gso, weight, bias, out):
         w_raw = keep.tile([P, PACK, CH], BF16)
         bias_bf = keep.tile([P, 1], BF16)
         gso_rows = []
-        for a in range(CHUNKS):
-            gso_chunk = rows.tile([P, PAIR, NODES], BF16, name="gso_chunk")
-            gso_rows.append(gso_chunk)
+        for t in range(TILES):
+            gso_tile = rows.tile([P, NODES], BF16, name="gso_tile")
+            gso_rows.append(gso_tile)
 
         nc.scalar.dma_start(
             out=w_raw[:], in_=weight.rearrange("o i j -> (o i) j").rearrange("(p t) j -> p t j", t=PACK)
         )
         nc.scalar.dma_start(out=bias_bf[:], in_=bias.rearrange("(c o) -> c o", o=1))
 
-        def load_gso(a):
-            for e in range(PAIR):
-                nc.sync.dma_start(out=gso_rows[a][:, e, :], in_=gso_split[a, e])
+        def load_gso(t):
+            nc.sync.dma_start(out=gso_rows[t][:], in_=gso_split[t // PAIR, t % PAIR])
 
         load_gso(0)
         for e in range(PAIR):
             nc.sync.dma_start(out=xs[:, :, e, 2 * CH : 3 * CH], in_=x2_split[e])
         load_gso(1)
         nc.sync.dma_start(out=x_sb[:], in_=x_cn)
+        load_gso(2)
         for e in range(PAIR):
             nc.sync.dma_start(out=xs[:, :, e, CH : 2 * CH], in_=x1_split[e])
-        for a in range(2, CHUNKS):
-            load_gso(a)
+        for t in range(3, TILES):
+            load_gso(t)
 
         bias_f32 = keep.tile([P, 1], F32)
         nc.vector.tensor_copy(out=bias_f32[:], in_=bias_bf[:])
@@ -99,7 +100,8 @@ def tile_graphconvlayer_pb_kernel(tc, x, x1, x2, gso, weight, bias, out):
         )
 
         x_words = x_sb[:].bitcast(F32)
-        xs_words = xs[:].bitcast(F32)
+        xs_tiles = xs[:].rearrange("p a e k -> p (a e) k")
+        xs_words = xs_tiles.bitcast(F32)
         gso_grouped = {}
         gso_codes = {}
         gso_scales = {}
@@ -109,35 +111,33 @@ def tile_graphconvlayer_pb_kernel(tc, x, x1, x2, gso, weight, bias, out):
         xs_scales = {}
         out_acc = {}
 
-        def transpose_gso(a):
-            words = gso_rows[a][:].bitcast(F32)
-            for e in range(PAIR):
-                grouped = work.tile([P, PASSES, P, PACK], BF16, name="gso_grouped", align_bytes=64, bufs=4)
-                grouped_words = grouped[:].bitcast(F32)
-                for half in range(PASSES // 2):
-                    bank = psum_gso.tile([P, 2, 2, P], F32, name="gso_bank")
-                    for g2 in range(2):
-                        for u in range(2):
-                            first = (4 * half + 2 * g2 + u) * P
-                            nc.tensor.transpose(bank[:, g2, u, :], words[:, e, first : first + P], ident[:])
-                    copy = nc.vector.tensor_copy if (e == PAIR - 1 and half == PASSES // 2 - 1) else nc.scalar.copy
-                    copy(
-                        out=grouped_words[:, 2 * half : 2 * half + 2],
-                        in_=bank[:].rearrange("q g u n -> q g n u"),
-                    )
-                gso_grouped[(a, e)] = grouped
-
-        def quantise_gso(a):
-            for e in range(PAIR):
-                codes = work.tile([P, PASSES, P], U32, name="gso_codes", align_bytes=64, bufs=6)
-                scales = work.tile([P, PASSES, P], U8, name="gso_scales", align_bytes=64, bufs=6)
-                nc.vector.quantize_mx(
-                    out=codes[:].rearrange("q g n -> q (g n)").bitcast(FP8X4),
-                    scales=scales[:].rearrange("q g n -> q (g n)"),
-                    in_=gso_grouped[(a, e)][:].rearrange("q g n t -> q (g n t)"),
+        def transpose_gso(t):
+            words = gso_rows[t][:].bitcast(F32)
+            grouped = work.tile([P, PASSES, P, PACK], BF16, name="gso_grouped", align_bytes=64)
+            grouped_words = grouped[:].bitcast(F32)
+            for half in range(PASSES // 2):
+                bank = psum_gso.tile([P, 2, 2, P], F32, name="gso_bank")
+                for g2 in range(2):
+                    for u in range(2):
+                        first = (4 * half + 2 * g2 + u) * P
+                        nc.tensor.transpose(bank[:, g2, u, :], words[:, first : first + P], ident[:])
+                copy = nc.vector.tensor_copy if (t % 2 == 1 and half == 1) else nc.scalar.copy
+                copy(
+                    out=grouped_words[:, 2 * half : 2 * half + 2],
+                    in_=bank[:].rearrange("q g u n -> q g n u"),
                 )
-                gso_codes[(a, e)] = codes
-                gso_scales[(a, e)] = scales
+            gso_grouped[t] = grouped
+
+        def quantise_gso(t):
+            codes = work.tile([P, PASSES, P], U32, name="gso_codes", align_bytes=64)
+            scales = work.tile([P, PASSES, P], U8, name="gso_scales", align_bytes=64)
+            nc.vector.quantize_mx(
+                out=codes[:].rearrange("q g n -> q (g n)").bitcast(FP8X4),
+                scales=scales[:].rearrange("q g n -> q (g n)"),
+                in_=gso_grouped[t][:].rearrange("q g n t -> q (g n t)"),
+            )
+            gso_codes[t] = codes
+            gso_scales[t] = scales
 
         def transpose_x(a):
             bank = psum_one.tile([P, CH], F32, name="x_bank")
@@ -146,89 +146,89 @@ def tile_graphconvlayer_pb_kernel(tc, x, x1, x2, gso, weight, bias, out):
                 out=xs[:, a, :, 0:CH], in_=bank[:].bitcast(BF16).rearrange("p (c e) -> p e c", e=PAIR)
             )
 
-        def first_matmul(a):
-            acc = psum_one.tile([P, PAIR, CH], F32, name="x3_acc")
-            for e in range(PAIR):
-                for g in range(PASSES):
-                    nc.tensor.matmul_mx(
-                        out=acc[:, e, :],
-                        lhsT=gso_codes[(a, e)][:, g, :].bitcast(FP8X4),
-                        lhsT_scale=gso_scales[(a, e)][:, g, :],
-                        rhs=x2_codes[:, g, :].bitcast(FP8X4),
-                        rhs_scale=x2_scales[:, g, :],
-                        start=(g == 0),
-                        stop=(g == PASSES - 1),
-                    )
-            x3_acc[a] = acc
+        def first_matmul(t):
+            acc = psum_one.tile([P, CH], F32, name="x3_acc")
+            for g in range(PASSES):
+                nc.tensor.matmul_mx(
+                    out=acc[:],
+                    lhsT=gso_codes[t][:, g, :].bitcast(FP8X4),
+                    lhsT_scale=gso_scales[t][:, g, :],
+                    rhs=x2_codes[:, g, :].bitcast(FP8X4),
+                    rhs_scale=x2_scales[:, g, :],
+                    start=(g == 0),
+                    stop=(g == PASSES - 1),
+                )
+            x3_acc[t] = acc
 
-        def finish_x3(a):
+        def finish_x3(t):
             nc.vector.scalar_tensor_tensor(
-                out=xs[:, a, :, 3 * CH : 4 * CH],
-                in0=x3_acc[a][:],
+                out=xs_tiles[:, t, 3 * CH : 4 * CH],
+                in0=x3_acc[t][:],
                 scalar=2.0,
-                in1=xs[:, a, :, CH : 2 * CH],
+                in1=xs_tiles[:, t, CH : 2 * CH],
                 op0=MULT,
                 op1=SUBTRACT,
             )
 
-        def transpose_xs(a):
-            bank = psum_one.tile([P, PAIR, 2, P], F32, name="xs_bank")
-            for e in range(PAIR):
-                for u in range(2):
-                    nc.tensor.transpose(bank[:, e, u, :], xs_words[:, a, e, u : K2 // 2 : 2], ident[:])
-            grouped = work.tile([P, CHUNK, PACK], BF16, name="xs_grouped", align_bytes=64)
-            nc.scalar.copy(
-                out=grouped[:].bitcast(F32).rearrange("q (p e) u -> q p e u", e=PAIR),
-                in_=bank[:].rearrange("q e u p -> q p e u"),
-            )
-            xs_grouped[a] = grouped
+        def transpose_xs(t):
+            bank = psum_one.tile([P, 2, P], F32, name="xs_bank")
+            for u in range(2):
+                nc.tensor.transpose(bank[:, u, :], xs_words[:, t, u : K2 // 2 : 2], ident[:])
+            grouped = work.tile([P, P, PACK], BF16, name="xs_grouped", align_bytes=64)
+            nc.scalar.copy(out=grouped[:].bitcast(F32), in_=bank[:].rearrange("q u p -> q p u"))
+            xs_grouped[t] = grouped
 
-        def quantise_xs(a):
-            codes = work.tile([P, CHUNK], U32, name="xs_codes", align_bytes=64)
-            scales = work.tile([P, CHUNK], U8, name="xs_scales", align_bytes=64)
+        def quantise_xs(t):
+            codes = work.tile([P, P], U32, name="xs_codes", align_bytes=64)
+            scales = work.tile([P, P], U8, name="xs_scales", align_bytes=64)
             nc.vector.quantize_mx(
-                out=codes[:].bitcast(FP8X4), scales=scales[:], in_=xs_grouped[a][:].rearrange("q n t -> q (n t)")
+                out=codes[:].bitcast(FP8X4), scales=scales[:], in_=xs_grouped[t][:].rearrange("q n t -> q (n t)")
             )
-            xs_codes[a] = codes
-            xs_scales[a] = scales
+            xs_codes[t] = codes
+            xs_scales[t] = scales
 
-        def second_matmul(a):
-            acc = psum_one.tile([P, CHUNK], F32, name="out_acc")
+        def second_matmul(t):
+            a, e = divmod(t, PAIR)
+            if e == 0:
+                out_acc[a] = psum_one.tile([P, PAIR, P], F32, name="out_acc")
             nc.tensor.matmul_mx(
-                out=acc[:],
+                out=out_acc[a][:, e, :],
                 lhsT=w_codes[:].bitcast(FP8X4),
                 lhsT_scale=w_scales[:],
-                rhs=xs_codes[a][:].bitcast(FP8X4),
-                rhs_scale=xs_scales[a][:],
+                rhs=xs_codes[t][:].bitcast(FP8X4),
+                rhs_scale=xs_scales[t][:],
                 start=True,
                 stop=True,
             )
-            out_acc[a] = acc
 
         def finish_out(a):
             nodes = slice(a * CHUNK, (a + 1) * CHUNK)
             result = work.tile([P, CHUNK], F32, name="result")
             nc.vector.scalar_tensor_tensor(
-                out=result[:], in0=out_acc[a][:], scalar=bias_f32[:, 0:1], in1=x_sb[:, nodes], op0=ADD, op1=ADD
+                out=result[:].rearrange("j (p e) -> j p e", e=PAIR),
+                in0=out_acc[a][:].rearrange("j e p -> j p e"),
+                scalar=bias_f32[:, 0:1],
+                in1=x_sb[:, nodes].rearrange("j (p e) -> j p e", e=PAIR),
+                op0=ADD,
+                op1=ADD,
             )
             nc.sync.dma_start(out=out_cn[:, nodes], in_=result[:])
 
-        for i in range(CHUNKS + 4):
-            if 0 <= i - 2 < CHUNKS:
-                finish_x3(i - 2)
-            if 0 <= i - 1 < CHUNKS:
-                quantise_gso(i - 1)
-            if 0 <= i - 3 < CHUNKS:
-                quantise_xs(i - 3)
-            if 0 <= i - 4 < CHUNKS:
-                finish_out(i - 4)
-            if i < CHUNKS:
-                transpose_gso(i)
-            if 0 <= i - 1 < CHUNKS:
-                transpose_x(i - 1)
-            if 0 <= i - 2 < CHUNKS:
-                transpose_xs(i - 2)
-            if 0 <= i - 1 < CHUNKS:
-                first_matmul(i - 1)
-            if 0 <= i - 3 < CHUNKS:
-                second_matmul(i - 3)
+        for h in range(TILES + 4):
+            if 0 <= h - 2 < TILES:
+                finish_x3(h - 2)
+            if 0 <= h - 1 < TILES:
+                quantise_gso(h - 1)
+            if h >= 5 and (h - 5) % PAIR == 0:
+                finish_out((h - 5) // PAIR)
+            if h < TILES:
+                transpose_gso(h)
+            if h % PAIR == 1 and h // PAIR < CHUNKS:
+                transpose_x(h // PAIR)
+            if 0 <= h - 2 < TILES:
+                transpose_xs(h - 2)
+                quantise_xs(h - 2)
+            if 0 <= h - 1 < TILES:
+                first_matmul(h - 1)
+            if 0 <= h - 3 < TILES:
+                second_matmul(h - 3)

@@ -22,7 +22,11 @@ PASSES = NODES // (P * PACK)
 PAIR = 2
 CHUNK = P * PAIR
 CHUNKS = NODES // CHUNK
-TILES = NODES // P
+HALF = K2 // 2
+X1_AT = 0
+X0_AT = CH
+X2_AT = CH + CH // 2
+X3_AT = HALF
 
 FLOPS = 2 * NODES * NODES * CH + 2 * NODES * K2 * CH
 
@@ -32,12 +36,12 @@ def tile_graphconvlayer_pb_kernel(tc, x, x1, x2, gso, weight, bias, out):
     x_cn = x[0, :, 0, :]
     out_cn = out[0, :, 0, :]
     x1_split = x1[0, 0, :, :].rearrange("(a p e) c -> e p a c", p=P, e=PAIR)
-    x2_split = x2[0, 0, :, :].rearrange("(a p e) c -> e p a c", p=P, e=PAIR)
+    x2_split = x2[0, 0, :, :].rearrange("(a p e) c -> p a (e c)", p=P, e=PAIR)
     gso_split = gso.rearrange("(a p e) m -> a e p m", p=P, e=PAIR)
 
     with ExitStack() as ctx:
         keep = ctx.enter_context(tc.tile_pool(name="keep", bufs=1))
-        rows = ctx.enter_context(tc.tile_pool(name="rows", bufs=TILES))
+        rows = ctx.enter_context(tc.tile_pool(name="rows", bufs=CHUNKS))
         work = ctx.enter_context(tc.tile_pool(name="work", bufs=3))
         psum_gso = ctx.enter_context(tc.psum_pool(name="psum_gso", bufs=4))
         psum_one = ctx.enter_context(tc.psum_pool(name="psum_one", bufs=1))
@@ -48,31 +52,32 @@ def tile_graphconvlayer_pb_kernel(tc, x, x1, x2, gso, weight, bias, out):
 
         xs = keep.tile([P, CHUNKS, PAIR, K2], BF16)
         x_sb = keep.tile([P, NODES], BF16)
+        x2_raw = keep.tile([P, CHUNKS, PAIR, CH], BF16)
         w_raw = keep.tile([P, PACK, CH], BF16)
         bias_bf = keep.tile([P, 1], BF16)
         gso_rows = []
-        for t in range(TILES):
-            gso_tile = rows.tile([P, NODES], BF16, name="gso_tile")
-            gso_rows.append(gso_tile)
+        for a in range(CHUNKS):
+            gso_chunk = rows.tile([P, PAIR, NODES], BF16, name="gso_chunk")
+            gso_rows.append(gso_chunk)
 
-        nc.scalar.dma_start(
-            out=w_raw[:], in_=weight.rearrange("o i j -> (o i) j").rearrange("(p t) j -> p t j", t=PACK)
-        )
+        nc.scalar.dma_start(out=w_raw[0:64, 0:2, :], in_=weight[1].rearrange("(q f) j -> q f j", f=2))
+        nc.scalar.dma_start(out=w_raw[0:64, 2:4, :], in_=weight[3].rearrange("(q f) j -> q f j", f=2))
+        nc.scalar.dma_start(out=w_raw[64:96, :, :], in_=weight[0].rearrange("(r t) j -> r t j", t=PACK))
+        nc.scalar.dma_start(out=w_raw[96:128, :, :], in_=weight[2].rearrange("(r t) j -> r t j", t=PACK))
         nc.scalar.dma_start(out=bias_bf[:], in_=bias.rearrange("(c o) -> c o", o=1))
 
-        def load_gso(t):
-            nc.sync.dma_start(out=gso_rows[t][:], in_=gso_split[t // PAIR, t % PAIR])
+        def load_gso(a):
+            for e in range(PAIR):
+                nc.sync.dma_start(out=gso_rows[a][:, e, :], in_=gso_split[a, e])
 
         load_gso(0)
-        for e in range(PAIR):
-            nc.sync.dma_start(out=xs[:, :, e, 2 * CH : 3 * CH], in_=x2_split[e])
+        nc.sync.dma_start(out=x2_raw[:].rearrange("p a e c -> p a (e c)"), in_=x2_split)
         load_gso(1)
         nc.sync.dma_start(out=x_sb[:], in_=x_cn)
-        load_gso(2)
         for e in range(PAIR):
-            nc.sync.dma_start(out=xs[:, :, e, CH : 2 * CH], in_=x1_split[e])
-        for t in range(3, TILES):
-            load_gso(t)
+            nc.sync.dma_start(out=xs[:, :, e, X1_AT : X1_AT + CH], in_=x1_split[e])
+        for a in range(2, CHUNKS):
+            load_gso(a)
 
         bias_f32 = keep.tile([P, 1], F32)
         nc.vector.tensor_copy(out=bias_f32[:], in_=bias_bf[:])
@@ -91,7 +96,7 @@ def tile_graphconvlayer_pb_kernel(tc, x, x1, x2, gso, weight, bias, out):
         for g in range(PASSES):
             nc.vector.tensor_copy(
                 out=x2_grouped[:, g].rearrange("p c (u e) -> p c u e", e=PAIR),
-                in_=xs[:, 2 * g : 2 * g + 2, :, 2 * CH : 3 * CH].rearrange("p u e c -> p c u e"),
+                in_=x2_raw[:, 2 * g : 2 * g + 2, :, :].rearrange("p u e c -> p c u e"),
             )
         nc.vector.quantize_mx(
             out=x2_codes[:].rearrange("p g c -> p (g c)").bitcast(FP8X4),
@@ -100,8 +105,12 @@ def tile_graphconvlayer_pb_kernel(tc, x, x1, x2, gso, weight, bias, out):
         )
 
         x_words = x_sb[:].bitcast(F32)
-        xs_tiles = xs[:].rearrange("p a e k -> p (a e) k")
-        xs_words = xs_tiles.bitcast(F32)
+        xs_words = xs[:].bitcast(F32)
+
+        nc.vector.tensor_copy(
+            out=xs_words.rearrange("p a e (u w) -> p (a e) u w", u=2)[:, :, :, X2_AT // 2 : X2_AT // 2 + CH // PACK],
+            in_=x2_raw[:].bitcast(F32).rearrange("p a e (r u) -> p (a e) u r", u=2),
+        )
         gso_grouped = {}
         gso_codes = {}
         gso_scales = {}
@@ -111,124 +120,130 @@ def tile_graphconvlayer_pb_kernel(tc, x, x1, x2, gso, weight, bias, out):
         xs_scales = {}
         out_acc = {}
 
-        def transpose_gso(t):
-            words = gso_rows[t][:].bitcast(F32)
-            grouped = work.tile([P, PASSES, P, PACK], BF16, name="gso_grouped", align_bytes=64)
-            grouped_words = grouped[:].bitcast(F32)
-            for half in range(PASSES // 2):
-                bank = psum_gso.tile([P, 2, 2, P], F32, name="gso_bank")
-                for g2 in range(2):
-                    for u in range(2):
-                        first = (4 * half + 2 * g2 + u) * P
-                        nc.tensor.transpose(bank[:, g2, u, :], words[:, first : first + P], ident[:])
-                copy = nc.vector.tensor_copy if (t % 2 == 1 and half == 1) else nc.scalar.copy
-                copy(
-                    out=grouped_words[:, 2 * half : 2 * half + 2],
-                    in_=bank[:].rearrange("q g u n -> q g n u"),
-                )
-            gso_grouped[t] = grouped
+        def transpose_gso(a):
+            words = gso_rows[a][:].bitcast(F32)
+            for e in range(PAIR):
+                grouped = work.tile([P, PASSES, P, PACK], BF16, name="gso_grouped", align_bytes=64, bufs=4)
+                grouped_words = grouped[:].bitcast(F32)
+                for half in range(PASSES // 2):
+                    bank = psum_gso.tile([P, 2, 2, P], F32, name="gso_bank")
+                    for g2 in range(2):
+                        for u in range(2):
+                            first = (4 * half + 2 * g2 + u) * P
+                            nc.tensor.transpose(bank[:, g2, u, :], words[:, e, first : first + P], ident[:])
+                    copy = nc.vector.tensor_copy if (e == PAIR - 1 and half == PASSES // 2 - 1) else nc.scalar.copy
+                    copy(
+                        out=grouped_words[:, 2 * half : 2 * half + 2],
+                        in_=bank[:].rearrange("q g u n -> q g n u"),
+                    )
+                gso_grouped[(a, e)] = grouped
 
-        def quantise_gso(t):
-            codes = work.tile([P, PASSES, P], U32, name="gso_codes", align_bytes=64)
-            scales = work.tile([P, PASSES, P], U8, name="gso_scales", align_bytes=64)
-            nc.vector.quantize_mx(
-                out=codes[:].rearrange("q g n -> q (g n)").bitcast(FP8X4),
-                scales=scales[:].rearrange("q g n -> q (g n)"),
-                in_=gso_grouped[t][:].rearrange("q g n t -> q (g n t)"),
-            )
-            gso_codes[t] = codes
-            gso_scales[t] = scales
+        def quantise_gso(a):
+            for e in range(PAIR):
+                codes = work.tile([P, PASSES, P], U32, name="gso_codes", align_bytes=64, bufs=6)
+                scales = work.tile([P, PASSES, P], U8, name="gso_scales", align_bytes=64, bufs=6)
+                nc.vector.quantize_mx(
+                    out=codes[:].rearrange("q g n -> q (g n)").bitcast(FP8X4),
+                    scales=scales[:].rearrange("q g n -> q (g n)"),
+                    in_=gso_grouped[(a, e)][:].rearrange("q g n t -> q (g n t)"),
+                )
+                gso_codes[(a, e)] = codes
+                gso_scales[(a, e)] = scales
 
         def transpose_x(a):
             bank = psum_one.tile([P, CH], F32, name="x_bank")
             nc.tensor.transpose(bank[:], x_words[:, a * P : (a + 1) * P], ident[:])
-            nc.scalar.copy(
-                out=xs[:, a, :, 0:CH], in_=bank[:].bitcast(BF16).rearrange("p (c e) -> p e c", e=PAIR)
-            )
-
-        def first_matmul(t):
-            acc = psum_one.tile([P, CH], F32, name="x3_acc")
-            for g in range(PASSES):
-                nc.tensor.matmul_mx(
-                    out=acc[:],
-                    lhsT=gso_codes[t][:, g, :].bitcast(FP8X4),
-                    lhsT_scale=gso_scales[t][:, g, :],
-                    rhs=x2_codes[:, g, :].bitcast(FP8X4),
-                    rhs_scale=x2_scales[:, g, :],
-                    start=(g == 0),
-                    stop=(g == PASSES - 1),
+            values = bank[:].bitcast(BF16).rearrange("p (r u f e) -> p e u r f", u=2, f=2, e=PAIR)
+            for e in range(PAIR):
+                halves = xs[:, a, e, :].rearrange("p (u s) -> p u s", u=2)
+                nc.scalar.copy(
+                    out=halves[:, :, X0_AT : X0_AT + CH // 2].rearrange("p u (r f) -> p u r f", f=2),
+                    in_=values[:, e],
                 )
-            x3_acc[t] = acc
 
-        def finish_x3(t):
+        def first_matmul(a):
+            acc = psum_one.tile([P, PAIR, CH], F32, name="x3_acc")
+            for e in range(PAIR):
+                for g in range(PASSES):
+                    nc.tensor.matmul_mx(
+                        out=acc[:, e, :],
+                        lhsT=gso_codes[(a, e)][:, g, :].bitcast(FP8X4),
+                        lhsT_scale=gso_scales[(a, e)][:, g, :],
+                        rhs=x2_codes[:, g, :].bitcast(FP8X4),
+                        rhs_scale=x2_scales[:, g, :],
+                        start=(g == 0),
+                        stop=(g == PASSES - 1),
+                    )
+            x3_acc[a] = acc
+
+        def finish_x3(a):
             nc.vector.scalar_tensor_tensor(
-                out=xs_tiles[:, t, 3 * CH : 4 * CH],
-                in0=x3_acc[t][:],
+                out=xs[:, a, :, X3_AT : X3_AT + CH],
+                in0=x3_acc[a][:],
                 scalar=2.0,
-                in1=xs_tiles[:, t, CH : 2 * CH],
+                in1=xs[:, a, :, X1_AT : X1_AT + CH],
                 op0=MULT,
                 op1=SUBTRACT,
             )
 
-        def transpose_xs(t):
-            bank = psum_one.tile([P, 2, P], F32, name="xs_bank")
-            for u in range(2):
-                nc.tensor.transpose(bank[:, u, :], xs_words[:, t, u : K2 // 2 : 2], ident[:])
-            grouped = work.tile([P, P, PACK], BF16, name="xs_grouped", align_bytes=64)
-            nc.scalar.copy(out=grouped[:].bitcast(F32), in_=bank[:].rearrange("q u p -> q p u"))
-            xs_grouped[t] = grouped
-
-        def quantise_xs(t):
-            codes = work.tile([P, P], U32, name="xs_codes", align_bytes=64)
-            scales = work.tile([P, P], U8, name="xs_scales", align_bytes=64)
-            nc.vector.quantize_mx(
-                out=codes[:].bitcast(FP8X4), scales=scales[:], in_=xs_grouped[t][:].rearrange("q n t -> q (n t)")
+        def transpose_xs(a):
+            bank = psum_one.tile([P, PAIR, 2, P], F32, name="xs_bank")
+            for e in range(PAIR):
+                for u in range(2):
+                    nc.tensor.transpose(bank[:, e, u, :], xs_words[:, a, e, u * P : (u + 1) * P], ident[:])
+            grouped = work.tile([P, CHUNK, PACK], BF16, name="xs_grouped", align_bytes=64)
+            nc.scalar.copy(
+                out=grouped[:].bitcast(F32).rearrange("q (p e) u -> q p e u", e=PAIR),
+                in_=bank[:].rearrange("q e u p -> q p e u"),
             )
-            xs_codes[t] = codes
-            xs_scales[t] = scales
+            xs_grouped[a] = grouped
 
-        def second_matmul(t):
-            a, e = divmod(t, PAIR)
-            if e == 0:
-                out_acc[a] = psum_one.tile([P, PAIR, P], F32, name="out_acc")
+        def quantise_xs(a):
+            codes = work.tile([P, CHUNK], U32, name="xs_codes", align_bytes=64)
+            scales = work.tile([P, CHUNK], U8, name="xs_scales", align_bytes=64)
+            nc.vector.quantize_mx(
+                out=codes[:].bitcast(FP8X4), scales=scales[:], in_=xs_grouped[a][:].rearrange("q n t -> q (n t)")
+            )
+            xs_codes[a] = codes
+            xs_scales[a] = scales
+
+        def second_matmul(a):
+            acc = psum_one.tile([P, CHUNK], F32, name="out_acc")
             nc.tensor.matmul_mx(
-                out=out_acc[a][:, e, :],
+                out=acc[:],
                 lhsT=w_codes[:].bitcast(FP8X4),
                 lhsT_scale=w_scales[:],
-                rhs=xs_codes[t][:].bitcast(FP8X4),
-                rhs_scale=xs_scales[t][:],
+                rhs=xs_codes[a][:].bitcast(FP8X4),
+                rhs_scale=xs_scales[a][:],
                 start=True,
                 stop=True,
             )
+            out_acc[a] = acc
 
         def finish_out(a):
             nodes = slice(a * CHUNK, (a + 1) * CHUNK)
             result = work.tile([P, CHUNK], F32, name="result")
             nc.vector.scalar_tensor_tensor(
-                out=result[:].rearrange("j (p e) -> j p e", e=PAIR),
-                in0=out_acc[a][:].rearrange("j e p -> j p e"),
-                scalar=bias_f32[:, 0:1],
-                in1=x_sb[:, nodes].rearrange("j (p e) -> j p e", e=PAIR),
-                op0=ADD,
-                op1=ADD,
+                out=result[:], in0=out_acc[a][:], scalar=bias_f32[:, 0:1], in1=x_sb[:, nodes], op0=ADD, op1=ADD
             )
             nc.sync.dma_start(out=out_cn[:, nodes], in_=result[:])
 
-        for h in range(TILES + 4):
-            if 0 <= h - 2 < TILES:
-                finish_x3(h - 2)
-            if 0 <= h - 1 < TILES:
-                quantise_gso(h - 1)
-            if h >= 5 and (h - 5) % PAIR == 0:
-                finish_out((h - 5) // PAIR)
-            if h < TILES:
-                transpose_gso(h)
-            if h % PAIR == 1 and h // PAIR < CHUNKS:
-                transpose_x(h // PAIR)
-            if 0 <= h - 2 < TILES:
-                transpose_xs(h - 2)
-                quantise_xs(h - 2)
-            if 0 <= h - 1 < TILES:
-                first_matmul(h - 1)
-            if 0 <= h - 3 < TILES:
-                second_matmul(h - 3)
+        for i in range(CHUNKS + 4):
+            if 0 <= i - 2 < CHUNKS:
+                finish_x3(i - 2)
+            if 0 <= i - 1 < CHUNKS:
+                quantise_gso(i - 1)
+            if 0 <= i - 3 < CHUNKS:
+                quantise_xs(i - 3)
+            if 0 <= i - 4 < CHUNKS:
+                finish_out(i - 4)
+            if i < CHUNKS:
+                transpose_gso(i)
+            if 0 <= i - 1 < CHUNKS:
+                transpose_x(i - 1)
+            if 0 <= i - 2 < CHUNKS:
+                transpose_xs(i - 2)
+            if 0 <= i - 1 < CHUNKS:
+                first_matmul(i - 1)
+            if 0 <= i - 3 < CHUNKS:
+                second_matmul(i - 3)

@@ -66,51 +66,68 @@ def tile_graphconvlayer_pb_kernel(tc, x, x1, x2, gso, weight, bias, out):
         nc.scalar.dma_start(out=w_raw[96:128, :, :], in_=weight[2].rearrange("(r t) j -> r t j", t=PACK))
         nc.scalar.dma_start(out=bias_bf[:], in_=bias.rearrange("(c o) -> c o", o=1))
 
+        def load_x1(n0, n1):
+            for e in range(PAIR):
+                nc.sync.dma_start(out=xs[:, n0:n1, e, X1_AT : X1_AT + CH], in_=x1_split[e][:, n0:n1])
+
+        def load_x(n0, n1):
+            nc.sync.dma_start(out=x_sb[:, n0 * CHUNK : n1 * CHUNK], in_=x_cn[:, n0 * CHUNK : n1 * CHUNK])
+
+        def load_x2():
+            nc.sync.dma_start(out=x2_raw[:].rearrange("p a e c -> p a (e c)"), in_=x2_split)
+
         def load_gso(a):
             for e in range(PAIR):
                 nc.sync.dma_start(out=gso_rows[a][:, e, :], in_=gso_split[a, e])
 
         load_gso(0)
-        nc.sync.dma_start(out=x2_raw[:].rearrange("p a e c -> p a (e c)"), in_=x2_split)
+        load_x2()
         load_gso(1)
-        nc.sync.dma_start(out=x_sb[:], in_=x_cn)
-        for e in range(PAIR):
-            nc.sync.dma_start(out=xs[:, :, e, X1_AT : X1_AT + CH], in_=x1_split[e])
-        for a in range(2, CHUNKS):
+        load_x1(0,4)
+        load_x(0,4)
+        load_gso(2)
+        load_gso(3)
+        load_x1(4,8)
+        load_x(4,8)
+        for a in range(4,8):
             load_gso(a)
-
-        bias_f32 = keep.tile([P, 1], F32)
-        nc.vector.tensor_copy(out=bias_f32[:], in_=bias_bf[:])
-
         w_grouped = keep.tile([P, CH, PACK], BF16, align_bytes=64)
         w_codes = keep.tile([P, CH], U32, align_bytes=64)
         w_scales = keep.tile([P, CH], U8, align_bytes=64)
-        nc.vector.tensor_copy(out=w_grouped[:], in_=w_raw[:].rearrange("p t j -> p j t"))
-        nc.vector.quantize_mx(
-            out=w_codes[:].bitcast(FP8X4), scales=w_scales[:], in_=w_grouped[:].rearrange("p j t -> p (j t)")
-        )
+
+        def quantise_weight():
+            nc.scalar.copy(out=w_grouped[:], in_=w_raw[:].rearrange("p t j -> p j t"))
+            nc.vector.quantize_mx(
+                out=w_codes[:].bitcast(FP8X4), scales=w_scales[:], in_=w_grouped[:].rearrange("p j t -> p (j t)")
+            )
 
         x2_grouped = keep.tile([P, PASSES, CH, PACK], BF16, align_bytes=64)
         x2_codes = keep.tile([P, PASSES, CH], U32, align_bytes=64)
         x2_scales = keep.tile([P, PASSES, CH], U8, align_bytes=64)
-        for g in range(PASSES):
-            nc.vector.tensor_copy(
-                out=x2_grouped[:, g].rearrange("p c (u e) -> p c u e", e=PAIR),
-                in_=x2_raw[:, 2 * g : 2 * g + 2, :, :].rearrange("p u e c -> p c u e"),
+
+        def quantise_x2():
+            for g in range(PASSES):
+                (nc.scalar.copy if g in (2, 3) else nc.vector.tensor_copy)(
+                    out=x2_grouped[:, g].rearrange("p c (u e) -> p c u e", e=PAIR),
+                    in_=x2_raw[:, 2 * g : 2 * g + 2, :, :].rearrange("p u e c -> p c u e"),
+                )
+            nc.vector.quantize_mx(
+                out=x2_codes[:].rearrange("p g c -> p (g c)").bitcast(FP8X4),
+                scales=x2_scales[:].rearrange("p g c -> p (g c)"),
+                in_=x2_grouped[:].rearrange("p g c t -> p (g c t)"),
             )
-        nc.vector.quantize_mx(
-            out=x2_codes[:].rearrange("p g c -> p (g c)").bitcast(FP8X4),
-            scales=x2_scales[:].rearrange("p g c -> p (g c)"),
-            in_=x2_grouped[:].rearrange("p g c t -> p (g c t)"),
-        )
 
         x_words = x_sb[:].bitcast(F32)
         xs_words = xs[:].bitcast(F32)
 
-        nc.vector.tensor_copy(
-            out=xs_words.rearrange("p a e (u w) -> p (a e) u w", u=2)[:, :, :, X2_AT // 2 : X2_AT // 2 + CH // PACK],
-            in_=x2_raw[:].bitcast(F32).rearrange("p a e (r u) -> p (a e) u r", u=2),
-        )
+        def place_x2(a0, a1):
+            nc.vector.tensor_copy(
+                out=xs_words[:, a0:a1].rearrange("p a e (u w) -> p (a e) u w", u=2)[
+                    :, :, :, X2_AT // 2 : X2_AT // 2 + CH // PACK
+                ],
+                in_=x2_raw[:, a0:a1].bitcast(F32).rearrange("p a e (r u) -> p (a e) u r", u=2),
+            )
+
         gso_grouped = {}
         gso_codes = {}
         gso_scales = {}
@@ -120,9 +137,12 @@ def tile_graphconvlayer_pb_kernel(tc, x, x1, x2, gso, weight, bias, out):
         xs_scales = {}
         out_acc = {}
 
-        def transpose_gso(a):
+        def on_vector(a, e, half):
+            return (a == 0 and half == 1) or (a > 1 and a % 2 == 0 and e == 1 and half == 1)
+
+        def transpose_gso(a, es=(0, 1)):
             words = gso_rows[a][:].bitcast(F32)
-            for e in range(PAIR):
+            for e in es:
                 grouped = work.tile([P, PASSES, P, PACK], BF16, name="gso_grouped", align_bytes=64, bufs=4)
                 grouped_words = grouped[:].bitcast(F32)
                 for half in range(PASSES // 2):
@@ -131,15 +151,15 @@ def tile_graphconvlayer_pb_kernel(tc, x, x1, x2, gso, weight, bias, out):
                         for u in range(2):
                             first = (4 * half + 2 * g2 + u) * P
                             nc.tensor.transpose(bank[:, g2, u, :], words[:, e, first : first + P], ident[:])
-                    copy = nc.vector.tensor_copy if (e == PAIR - 1 and half == PASSES // 2 - 1) else nc.scalar.copy
+                    copy = nc.vector.tensor_copy if on_vector(a, e, half) else nc.scalar.copy
                     copy(
                         out=grouped_words[:, 2 * half : 2 * half + 2],
                         in_=bank[:].rearrange("q g u n -> q g n u"),
                     )
                 gso_grouped[(a, e)] = grouped
 
-        def quantise_gso(a):
-            for e in range(PAIR):
+        def quantise_gso(a, es=(0, 1)):
+            for e in es:
                 codes = work.tile([P, PASSES, P], U32, name="gso_codes", align_bytes=64, bufs=6)
                 scales = work.tile([P, PASSES, P], U8, name="gso_scales", align_bytes=64, bufs=6)
                 nc.vector.quantize_mx(
@@ -161,9 +181,11 @@ def tile_graphconvlayer_pb_kernel(tc, x, x1, x2, gso, weight, bias, out):
                     in_=values[:, e],
                 )
 
-        def first_matmul(a):
-            acc = psum_one.tile([P, PAIR, CH], F32, name="x3_acc")
-            for e in range(PAIR):
+        def first_matmul(a, es=(0, 1)):
+            if 0 in es:
+                x3_acc[a] = psum_one.tile([P, PAIR, CH], F32, name="x3_acc")
+            acc = x3_acc[a]
+            for e in es:
                 for g in range(PASSES):
                     nc.tensor.matmul_mx(
                         out=acc[:, e, :],
@@ -174,7 +196,6 @@ def tile_graphconvlayer_pb_kernel(tc, x, x1, x2, gso, weight, bias, out):
                         start=(g == 0),
                         stop=(g == PASSES - 1),
                     )
-            x3_acc[a] = acc
 
         def finish_x3(a):
             nc.vector.scalar_tensor_tensor(
@@ -224,15 +245,25 @@ def tile_graphconvlayer_pb_kernel(tc, x, x1, x2, gso, weight, bias, out):
             nodes = slice(a * CHUNK, (a + 1) * CHUNK)
             result = work.tile([P, CHUNK], F32, name="result")
             nc.vector.scalar_tensor_tensor(
-                out=result[:], in0=out_acc[a][:], scalar=bias_f32[:, 0:1], in1=x_sb[:, nodes], op0=ADD, op1=ADD
+                out=result[:], in0=out_acc[a][:], scalar=bias_bf[:, 0:1], in1=x_sb[:, nodes], op0=ADD, op1=ADD
             )
             nc.sync.dma_start(out=out_cn[:, nodes], in_=result[:])
 
-        for i in range(CHUNKS + 4):
+        transpose_gso(0)
+        quantise_x2()
+        quantise_weight()
+        quantise_gso(0)
+        transpose_gso(1)
+        first_matmul(0)
+        place_x2(0, 4)
+        transpose_x(0)
+        for i in range(2, CHUNKS + 4):
             if 0 <= i - 2 < CHUNKS:
                 finish_x3(i - 2)
             if 0 <= i - 1 < CHUNKS:
                 quantise_gso(i - 1)
+            if i == 4:
+                place_x2(4, 8)
             if 0 <= i - 3 < CHUNKS:
                 quantise_xs(i - 3)
             if 0 <= i - 4 < CHUNKS:

@@ -96,7 +96,7 @@ def tile_graphconvlayer_pb_kernel(tc, x, x1, x2, gso, weight, bias, out):
         w_scales = keep.tile([P, CH], U8, align_bytes=64)
 
         def quantise_weight():
-            nc.scalar.copy(out=w_grouped[:], in_=w_raw[:].rearrange("p t j -> p j t"))
+            nc.vector.tensor_copy(out=w_grouped[:], in_=w_raw[:].rearrange("p t j -> p j t"))
             nc.vector.quantize_mx(
                 out=w_codes[:].bitcast(FP8X4), scales=w_scales[:], in_=w_grouped[:].rearrange("p j t -> p (j t)")
             )
@@ -107,7 +107,7 @@ def tile_graphconvlayer_pb_kernel(tc, x, x1, x2, gso, weight, bias, out):
 
         def quantise_x2():
             for g in range(PASSES):
-                (nc.scalar.copy if g in (2, 3) else nc.vector.tensor_copy)(
+                nc.vector.tensor_copy(
                     out=x2_grouped[:, g].rearrange("p c (u e) -> p c u e", e=PAIR),
                     in_=x2_raw[:, 2 * g : 2 * g + 2, :, :].rearrange("p u e c -> p c u e"),
                 )
@@ -138,7 +138,7 @@ def tile_graphconvlayer_pb_kernel(tc, x, x1, x2, gso, weight, bias, out):
         out_acc = {}
 
         def on_vector(a, e, half):
-            return (a == 0 and half == 1) or (a > 1 and a % 2 == 0 and e == 1 and half == 1)
+            return half == 1 and (a == 0 or e == 1)
 
         def transpose_gso(a, es=(0, 1)):
             words = gso_rows[a][:].bitcast(F32)

@@ -35,9 +35,9 @@ def tile_graphconvlayer_pb_kernel(tc, x, x1, x2, gso, weight, bias, out):
     nc = tc.nc
     x_cn = x[0, :, 0, :]
     out_cn = out[0, :, 0, :]
-    x1_split = x1[0, 0, :, :].rearrange("(a p e) c -> e p a c", p=P, e=PAIR)
+    x1_split = x1[0, 0, :, :].rearrange("(a p e) c -> p a (e c)", p=P, e=PAIR)
     x2_split = x2[0, 0, :, :].rearrange("(a p e) c -> p a (e c)", p=P, e=PAIR)
-    gso_split = gso.rearrange("(a p e) m -> a e p m", p=P, e=PAIR)
+    gso_split = gso.rearrange("(a p e) m -> a p e m", p=P, e=PAIR)
 
     with ExitStack() as ctx:
         keep = ctx.enter_context(tc.tile_pool(name="keep", bufs=1))
@@ -53,6 +53,7 @@ def tile_graphconvlayer_pb_kernel(tc, x, x1, x2, gso, weight, bias, out):
         xs = keep.tile([P, CHUNKS, PAIR, K2], BF16)
         x_sb = keep.tile([P, NODES], BF16)
         x2_raw = keep.tile([P, CHUNKS, PAIR, CH], BF16)
+        x1_raw = keep.tile([P, CHUNKS, PAIR, CH], BF16)
         w_raw = keep.tile([P, PACK, CH], BF16)
         bias_bf = keep.tile([P, 1], BF16)
         gso_rows = []
@@ -67,8 +68,9 @@ def tile_graphconvlayer_pb_kernel(tc, x, x1, x2, gso, weight, bias, out):
         nc.scalar.dma_start(out=bias_bf[:], in_=bias.rearrange("(c o) -> c o", o=1))
 
         def load_x1(n0, n1):
-            for e in range(PAIR):
-                nc.sync.dma_start(out=xs[:, n0:n1, e, X1_AT : X1_AT + CH], in_=x1_split[e][:, n0:n1])
+            nc.sync.dma_start(
+                out=x1_raw[:, n0:n1].rearrange("p a e c -> p a (e c)"), in_=x1_split[:, n0:n1]
+            )
 
         def load_x(n0, n1):
             nc.sync.dma_start(out=x_sb[:, n0 * CHUNK : n1 * CHUNK], in_=x_cn[:, n0 * CHUNK : n1 * CHUNK])
@@ -77,19 +79,18 @@ def tile_graphconvlayer_pb_kernel(tc, x, x1, x2, gso, weight, bias, out):
             nc.sync.dma_start(out=x2_raw[:].rearrange("p a e c -> p a (e c)"), in_=x2_split)
 
         def load_gso(a):
-            for e in range(PAIR):
-                nc.sync.dma_start(out=gso_rows[a][:, e, :], in_=gso_split[a, e])
+            if a in (0, CHUNKS - 1):
+                for e in range(PAIR):
+                    nc.sync.dma_start(out=gso_rows[a][:, e, :], in_=gso_split[a, :, e, :])
+            else:
+                nc.sync.dma_start(out=gso_rows[a][:], in_=gso_split[a])
 
         load_gso(0)
         load_x2()
         load_gso(1)
-        load_x1(0,4)
-        load_x(0,4)
-        load_gso(2)
-        load_gso(3)
-        load_x1(4,8)
-        load_x(4,8)
-        for a in range(4,8):
+        load_x1(0, CHUNKS)
+        load_x(0, CHUNKS)
+        for a in range(2, CHUNKS):
             load_gso(a)
         w_grouped = keep.tile([P, CH, PACK], BF16, align_bytes=64)
         w_codes = keep.tile([P, CH], U32, align_bytes=64)
@@ -119,6 +120,9 @@ def tile_graphconvlayer_pb_kernel(tc, x, x1, x2, gso, weight, bias, out):
 
         x_words = x_sb[:].bitcast(F32)
         xs_words = xs[:].bitcast(F32)
+
+        def place_x1(a0, a1):
+            nc.vector.tensor_copy(out=xs[:, a0:a1, :, X1_AT : X1_AT + CH], in_=x1_raw[:, a0:a1])
 
         def place_x2(a0, a1):
             nc.vector.tensor_copy(
@@ -202,7 +206,7 @@ def tile_graphconvlayer_pb_kernel(tc, x, x1, x2, gso, weight, bias, out):
                 out=xs[:, a, :, X3_AT : X3_AT + CH],
                 in0=x3_acc[a][:],
                 scalar=2.0,
-                in1=xs[:, a, :, X1_AT : X1_AT + CH],
+                in1=x1_raw[:, a],
                 op0=MULT,
                 op1=SUBTRACT,
             )
@@ -255,15 +259,14 @@ def tile_graphconvlayer_pb_kernel(tc, x, x1, x2, gso, weight, bias, out):
         quantise_gso(0)
         transpose_gso(1)
         first_matmul(0)
-        place_x2(0, 4)
+        place_x2(0, CHUNKS)
+        place_x1(0, CHUNKS)
         transpose_x(0)
         for i in range(2, CHUNKS + 4):
             if 0 <= i - 2 < CHUNKS:
                 finish_x3(i - 2)
             if 0 <= i - 1 < CHUNKS:
                 quantise_gso(i - 1)
-            if i == 4:
-                place_x2(4, 8)
             if 0 <= i - 3 < CHUNKS:
                 quantise_xs(i - 3)
             if 0 <= i - 4 < CHUNKS:

@@ -79,11 +79,8 @@ def tile_graphconvlayer_pb_kernel(tc, x, x1, x2, gso, weight, bias, out):
             nc.sync.dma_start(out=x2_raw[:].rearrange("p a e c -> p a (e c)"), in_=x2_split)
 
         def load_gso(a):
-            if a in (0, CHUNKS - 1):
-                for e in range(PAIR):
-                    nc.sync.dma_start(out=gso_rows[a][:, e, :], in_=gso_split[a, :, e, :])
-            else:
-                nc.sync.dma_start(out=gso_rows[a][:], in_=gso_split[a])
+            for e in range(PAIR):
+                nc.sync.dma_start(out=gso_rows[a][:, e, :], in_=gso_split[a, :, e, :])
 
         load_gso(0)
         load_x2()
@@ -97,7 +94,7 @@ def tile_graphconvlayer_pb_kernel(tc, x, x1, x2, gso, weight, bias, out):
         w_scales = keep.tile([P, CH], U8, align_bytes=64)
 
         def quantise_weight():
-            nc.vector.tensor_copy(out=w_grouped[:], in_=w_raw[:].rearrange("p t j -> p j t"))
+            nc.scalar.copy(out=w_grouped[:], in_=w_raw[:].rearrange("p t j -> p j t"))
             nc.vector.quantize_mx(
                 out=w_codes[:].bitcast(FP8X4), scales=w_scales[:], in_=w_grouped[:].rearrange("p j t -> p (j t)")
             )
@@ -108,7 +105,7 @@ def tile_graphconvlayer_pb_kernel(tc, x, x1, x2, gso, weight, bias, out):
 
         def quantise_x2():
             for g in range(PASSES):
-                nc.vector.tensor_copy(
+                (nc.vector.tensor_copy if g < 2 else nc.scalar.copy)(
                     out=x2_grouped[:, g].rearrange("p c (u e) -> p c u e", e=PAIR),
                     in_=x2_raw[:, 2 * g : 2 * g + 2, :, :].rearrange("p u e c -> p c u e"),
                 )
@@ -140,144 +137,180 @@ def tile_graphconvlayer_pb_kernel(tc, x, x1, x2, gso, weight, bias, out):
         xs_codes = {}
         xs_scales = {}
         out_acc = {}
+        x3_pair = {}
+        LAST = CHUNKS - 1
 
-        def on_vector(a, e, half):
-            return half == 1 and (a == 0 or e == 1)
-
-        def transpose_gso(a, es=(0, 1)):
+        def transpose_gso(a, e, copies):
             words = gso_rows[a][:].bitcast(F32)
-            for e in es:
-                grouped = work.tile([P, PASSES, P, PACK], BF16, name="gso_grouped", align_bytes=64, bufs=4)
-                grouped_words = grouped[:].bitcast(F32)
-                for half in range(PASSES // 2):
-                    bank = psum_gso.tile([P, 2, 2, P], F32, name="gso_bank")
-                    for g2 in range(2):
-                        for u in range(2):
-                            first = (4 * half + 2 * g2 + u) * P
-                            nc.tensor.transpose(bank[:, g2, u, :], words[:, e, first : first + P], ident[:])
-                    copy = nc.vector.tensor_copy if on_vector(a, e, half) else nc.scalar.copy
-                    copy(
-                        out=grouped_words[:, 2 * half : 2 * half + 2],
-                        in_=bank[:].rearrange("q g u n -> q g n u"),
-                    )
-                gso_grouped[(a, e)] = grouped
+            grouped = work.tile([P, PASSES, P, PACK], BF16, name="gso_grouped", align_bytes=64, bufs=4)
+            grouped_words = grouped[:].bitcast(F32)
+            for half in range(PASSES // 2):
+                bank = psum_gso.tile([P, 2, 2, P], F32, name="gso_bank")
+                for g2 in range(2):
+                    for u in range(2):
+                        first = (4 * half + 2 * g2 + u) * P
+                        nc.tensor.transpose(bank[:, g2, u, :], words[:, e, first : first + P], ident[:])
+                copies[half](
+                    out=grouped_words[:, 2 * half : 2 * half + 2],
+                    in_=bank[:].rearrange("q g u n -> q g n u"),
+                )
+            gso_grouped[(a, e)] = grouped
 
-        def quantise_gso(a, es=(0, 1)):
-            for e in es:
-                codes = work.tile([P, PASSES, P], U32, name="gso_codes", align_bytes=64, bufs=6)
-                scales = work.tile([P, PASSES, P], U8, name="gso_scales", align_bytes=64, bufs=6)
+        def quantise_gso(a, e, parts=1):
+            codes = work.tile([P, PASSES, P], U32, name="gso_codes", align_bytes=64, bufs=6)
+            scales = work.tile([P, PASSES, P], U8, name="gso_scales", align_bytes=64, bufs=6)
+            for part in range(parts):
+                g = slice(part * PASSES // parts, (part + 1) * PASSES // parts)
                 nc.vector.quantize_mx(
-                    out=codes[:].rearrange("q g n -> q (g n)").bitcast(FP8X4),
-                    scales=scales[:].rearrange("q g n -> q (g n)"),
-                    in_=gso_grouped[(a, e)][:].rearrange("q g n t -> q (g n t)"),
+                    out=codes[:, g].rearrange("q g n -> q (g n)").bitcast(FP8X4),
+                    scales=scales[:, g].rearrange("q g n -> q (g n)"),
+                    in_=gso_grouped[(a, e)][:, g].rearrange("q g n t -> q (g n t)"),
                 )
-                gso_codes[(a, e)] = codes
-                gso_scales[(a, e)] = scales
+            gso_codes[(a, e)] = codes
+            gso_scales[(a, e)] = scales
 
-        def transpose_x(a):
-            bank = psum_one.tile([P, CH], F32, name="x_bank")
-            nc.tensor.transpose(bank[:], x_words[:, a * P : (a + 1) * P], ident[:])
-            values = bank[:].bitcast(BF16).rearrange("p (r u f e) -> p e u r f", u=2, f=2, e=PAIR)
-            for e in range(PAIR):
-                halves = xs[:, a, e, :].rearrange("p (u s) -> p u s", u=2)
-                nc.scalar.copy(
-                    out=halves[:, :, X0_AT : X0_AT + CH // 2].rearrange("p u (r f) -> p u r f", f=2),
-                    in_=values[:, e],
-                )
-
-        def first_matmul(a, es=(0, 1)):
-            if 0 in es:
-                x3_acc[a] = psum_one.tile([P, PAIR, CH], F32, name="x3_acc")
-            acc = x3_acc[a]
-            for e in es:
-                for g in range(PASSES):
-                    nc.tensor.matmul_mx(
-                        out=acc[:, e, :],
-                        lhsT=gso_codes[(a, e)][:, g, :].bitcast(FP8X4),
-                        lhsT_scale=gso_scales[(a, e)][:, g, :],
-                        rhs=x2_codes[:, g, :].bitcast(FP8X4),
-                        rhs_scale=x2_scales[:, g, :],
-                        start=(g == 0),
-                        stop=(g == PASSES - 1),
+        def transpose_x(chunks):
+            bank = psum_one.tile([P, len(chunks), CH], F32, name="x_bank")
+            for i, a in enumerate(chunks):
+                nc.tensor.transpose(bank[:, i], x_words[:, a * P : (a + 1) * P], ident[:])
+            for i, a in enumerate(chunks):
+                values = bank[:, i].bitcast(BF16).rearrange("p (r u f e) -> p e u r f", u=2, f=2, e=PAIR)
+                for e in range(PAIR):
+                    halves = xs[:, a, e, :].rearrange("p (u s) -> p u s", u=2)
+                    nc.scalar.copy(
+                        out=halves[:, :, X0_AT : X0_AT + CH // 2].rearrange("p u (r f) -> p u r f", f=2),
+                        in_=values[:, e],
                     )
 
-        def finish_x3(a):
+        def first_matmul(a, e):
+            if a == LAST:
+                acc = psum_gso.tile([P, 1, CH], F32, name="gso_bank")
+                x3_acc[(a, e)] = acc[:]
+            else:
+                if e == 0:
+                    x3_pair[a] = psum_one.tile([P, PAIR, CH], F32, name="x3_acc")
+                acc = x3_pair[a]
+                x3_acc[(a, e)] = acc[:, e : e + 1]
+            for g in range(PASSES):
+                nc.tensor.matmul_mx(
+                    out=x3_acc[(a, e)][:, 0],
+                    lhsT=gso_codes[(a, e)][:, g, :].bitcast(FP8X4),
+                    lhsT_scale=gso_scales[(a, e)][:, g, :],
+                    rhs=x2_codes[:, g, :].bitcast(FP8X4),
+                    rhs_scale=x2_scales[:, g, :],
+                    start=(g == 0),
+                    stop=(g == PASSES - 1),
+                )
+
+        def finish_x3(a, es=(0, 1)):
             nc.vector.scalar_tensor_tensor(
-                out=xs[:, a, :, X3_AT : X3_AT + CH],
-                in0=x3_acc[a][:],
+                out=xs[:, a, es[0] : es[-1] + 1, X3_AT : X3_AT + CH],
+                in0=x3_pair[a][:] if a < LAST else x3_acc[(a, es[0])],
                 scalar=2.0,
-                in1=x1_raw[:, a],
+                in1=x1_raw[:, a, es[0] : es[-1] + 1],
                 op0=MULT,
                 op1=SUBTRACT,
             )
 
-        def transpose_xs(a):
-            bank = psum_one.tile([P, PAIR, 2, P], F32, name="xs_bank")
-            for e in range(PAIR):
+        def transpose_xs(a, es=(0, 1)):
+            if a < LAST:
+                bank = psum_one.tile([P, len(es), 2, P], F32, name="xs_bank")
+            else:
+                bank = psum_gso.tile([P, len(es), 2, P], F32, name="gso_bank")
+            for i, e in enumerate(es):
                 for u in range(2):
-                    nc.tensor.transpose(bank[:, e, u, :], xs_words[:, a, e, u * P : (u + 1) * P], ident[:])
-            grouped = work.tile([P, CHUNK, PACK], BF16, name="xs_grouped", align_bytes=64)
+                    nc.tensor.transpose(bank[:, i, u, :], xs_words[:, a, e, u * P : (u + 1) * P], ident[:])
+            grouped = work.tile([P, len(es), P, PACK], BF16, name="xs_grouped", align_bytes=64, bufs=5)
             nc.scalar.copy(
-                out=grouped[:].bitcast(F32).rearrange("q (p e) u -> q p e u", e=PAIR),
-                in_=bank[:].rearrange("q e u p -> q p e u"),
+                out=grouped[:].bitcast(F32),
+                in_=bank[:].rearrange("q e u p -> q e p u"),
             )
-            xs_grouped[a] = grouped
+            xs_grouped[(a, es)] = grouped
 
-        def quantise_xs(a):
-            codes = work.tile([P, CHUNK], U32, name="xs_codes", align_bytes=64)
-            scales = work.tile([P, CHUNK], U8, name="xs_scales", align_bytes=64)
+        def quantise_xs(a, es=(0, 1)):
+            codes = work.tile([P, len(es) * P], U32, name="xs_codes", align_bytes=64, bufs=5)
+            scales = work.tile([P, len(es) * P], U8, name="xs_scales", align_bytes=64, bufs=5)
             nc.vector.quantize_mx(
-                out=codes[:].bitcast(FP8X4), scales=scales[:], in_=xs_grouped[a][:].rearrange("q n t -> q (n t)")
+                out=codes[:].bitcast(FP8X4), scales=scales[:], in_=xs_grouped[(a, es)][:].rearrange("q e p t -> q (e p t)")
             )
-            xs_codes[a] = codes
-            xs_scales[a] = scales
+            xs_codes[(a, es)] = codes
+            xs_scales[(a, es)] = scales
 
-        def second_matmul(a):
-            acc = psum_one.tile([P, CHUNK], F32, name="out_acc")
+        def second_matmul(a, es=(0, 1)):
+            if a < LAST:
+                out_acc[a] = psum_one.tile([P, PAIR, P], F32, name="out_acc")
+            elif 0 in es:
+                out_acc[a] = psum_gso.tile([P, PAIR, P], F32, name="gso_bank")
             nc.tensor.matmul_mx(
-                out=acc[:],
+                out=out_acc[a][:, es[0] : es[-1] + 1, :].rearrange("j e p -> j (e p)"),
                 lhsT=w_codes[:].bitcast(FP8X4),
                 lhsT_scale=w_scales[:],
-                rhs=xs_codes[a][:].bitcast(FP8X4),
-                rhs_scale=xs_scales[a][:],
+                rhs=xs_codes[(a, es)][:].bitcast(FP8X4),
+                rhs_scale=xs_scales[(a, es)][:],
                 start=True,
                 stop=True,
             )
-            out_acc[a] = acc
 
         def finish_out(a):
             nodes = slice(a * CHUNK, (a + 1) * CHUNK)
-            result = work.tile([P, CHUNK], F32, name="result")
+            result = work.tile([P, P, PAIR], F32, name="result", bufs=4)
             nc.vector.scalar_tensor_tensor(
-                out=result[:], in0=out_acc[a][:], scalar=bias_bf[:, 0:1], in1=x_sb[:, nodes], op0=ADD, op1=ADD
+                out=result[:],
+                in0=out_acc[a][:].rearrange("j e p -> j p e"),
+                scalar=bias_bf[:, 0:1],
+                in1=x_sb[:, nodes].rearrange("j (p e) -> j p e", e=PAIR),
+                op0=ADD,
+                op1=ADD,
             )
-            nc.sync.dma_start(out=out_cn[:, nodes], in_=result[:])
+            nc.sync.dma_start(out=out_cn[:, nodes], in_=result[:].rearrange("j p e -> j (p e)"))
 
-        transpose_gso(0)
+        S, V = nc.scalar.copy, nc.vector.tensor_copy
+
+        transpose_gso(0, 0, (S, V))
+        transpose_gso(0, 1, (S, V))
         quantise_x2()
         quantise_weight()
-        quantise_gso(0)
-        transpose_gso(1)
-        first_matmul(0)
-        place_x2(0, CHUNKS)
-        place_x1(0, CHUNKS)
-        transpose_x(0)
-        for i in range(2, CHUNKS + 4):
-            if 0 <= i - 2 < CHUNKS:
+        for i in range(1, CHUNKS):
+            quantise_gso(i - 1, 0)
+            if i >= 2:
                 finish_x3(i - 2)
-            if 0 <= i - 1 < CHUNKS:
-                quantise_gso(i - 1)
-            if 0 <= i - 3 < CHUNKS:
-                quantise_xs(i - 3)
-            if 0 <= i - 4 < CHUNKS:
+            if i >= 4:
                 finish_out(i - 4)
-            if i < CHUNKS:
-                transpose_gso(i)
-            if 0 <= i - 1 < CHUNKS:
-                transpose_x(i - 1)
-            if 0 <= i - 2 < CHUNKS:
+            quantise_gso(i - 1, 1)
+            if i >= 3:
+                quantise_xs(i - 3)
+            transpose_gso(i, 0, (S, S))
+            transpose_gso(i, 1, (S, V if i % 2 == 1 and i < LAST else S))
+            if i >= 2:
                 transpose_xs(i - 2)
-            if 0 <= i - 1 < CHUNKS:
-                first_matmul(i - 1)
-            if 0 <= i - 3 < CHUNKS:
+            first_matmul(i - 1, 0)
+            first_matmul(i - 1, 1)
+            if i >= 3:
                 second_matmul(i - 3)
+            if i == 1:
+                place_x2(0, CHUNKS)
+                place_x1(0, CHUNKS)
+                transpose_x(range(4))
+                transpose_x(range(4, 8))
+        quantise_gso(7, 0)
+        first_matmul(7, 0)
+        quantise_gso(7, 1)
+        finish_x3(6)
+        first_matmul(7, 1)
+        transpose_xs(6)
+        finish_x3(7, (0,))
+        quantise_xs(5)
+        transpose_xs(7, (0,))
+        finish_x3(7, (1,))
+        finish_out(4)
+        transpose_xs(7, (1,))
+        second_matmul(5)
+        quantise_xs(6)
+        finish_out(5)
+        second_matmul(6)
+        quantise_xs(7, (0,))
+        second_matmul(7, (0,))
+        quantise_xs(7, (1,))
+        second_matmul(7, (1,))
+        finish_out(6)
+        finish_out(7)

@@ -78,17 +78,24 @@ def tile_graphconvlayer_pb_kernel(tc, x, x1, x2, gso, weight, bias, out):
         def load_x2():
             nc.sync.dma_start(out=x2_raw[:].rearrange("p a e c -> p a (e c)"), in_=x2_split)
 
-        def load_gso(a):
-            for e in range(PAIR):
+        def load_gso(a, es=(0, 1)):
+            for e in es:
                 nc.sync.dma_start(out=gso_rows[a][:, e, :], in_=gso_split[a, :, e, :])
 
         load_gso(0)
         load_x2()
         load_gso(1)
-        load_x1(0, CHUNKS)
-        load_x(0, CHUNKS)
-        for a in range(2, CHUNKS):
+        load_x1(0, 4)
+        load_x(0, 4)
+        for a in range(2, 6):
             load_gso(a)
+        load_x1(4, 6)
+        load_x(4, 6)
+        load_gso(6)
+        load_gso(7)
+        load_x1(6, 8)
+        load_x(6, 8)
+
         w_grouped = keep.tile([P, CH, PACK], BF16, align_bytes=64)
         w_codes = keep.tile([P, CH], U32, align_bytes=64)
         w_scales = keep.tile([P, CH], U8, align_bytes=64)
@@ -272,6 +279,9 @@ def tile_graphconvlayer_pb_kernel(tc, x, x1, x2, gso, weight, bias, out):
         quantise_weight()
         for i in range(1, CHUNKS):
             quantise_gso(i - 1, 0)
+            if i == 6:
+                place_x1(4, 6)
+                transpose_x(range(4, 6))
             if i >= 2:
                 finish_x3(i - 2)
             if i >= 4:
@@ -289,12 +299,13 @@ def tile_graphconvlayer_pb_kernel(tc, x, x1, x2, gso, weight, bias, out):
                 second_matmul(i - 3)
             if i == 1:
                 place_x2(0, CHUNKS)
-                place_x1(0, CHUNKS)
+                place_x1(0, 4)
                 transpose_x(range(4))
-                transpose_x(range(4, 8))
         quantise_gso(7, 0)
+        transpose_x(range(6, 8))
         first_matmul(7, 0)
-        quantise_gso(7, 1)
+        place_x1(6, 8)
+        quantise_gso(7, 1, 2)
         finish_x3(6)
         first_matmul(7, 1)
         transpose_xs(6)

from contextlib import ExitStack

import concourse.mybir as mybir
from concourse.masks import make_identity

BF16 = mybir.dt.bfloat16
F32 = mybir.dt.float32
U32 = mybir.dt.uint32
U8 = mybir.dt.uint8
FP8X4 = mybir.dt.float8_e4m3fn_x4
MULT = mybir.AluOpType.mult
ADD = mybir.AluOpType.add
SUBTRACT = mybir.AluOpType.subtract

P = 128
PACK = 4
NODES = 2048
CH = 128
ORDERS = 4
K2 = ORDERS * CH
PASSES = NODES // (P * PACK)
PAIR = 2
CHUNK = P * PAIR
CHUNKS = NODES // CHUNK
HALF = K2 // 2
X1_AT = 0
X0_AT = CH
X2_AT = CH + CH // 2
X3_AT = HALF

FLOPS = 2 * NODES * NODES * CH + 2 * NODES * K2 * CH


def tile_graphconvlayer_pb_kernel(tc, x, x1, x2, gso, weight, bias, out):
    nc = tc.nc
    x_cn = x[0, :, 0, :]
    out_cn = out[0, :, 0, :]
    x1_split = x1[0, 0, :, :].rearrange("(a p e) c -> p a (e c)", p=P, e=PAIR)
    x2_split = x2[0, 0, :, :].rearrange("(a p e) c -> p a (e c)", p=P, e=PAIR)
    gso_split = gso.rearrange("(a p e) m -> a p e m", p=P, e=PAIR)

    with ExitStack() as ctx:
        keep = ctx.enter_context(tc.tile_pool(name="keep", bufs=1))
        rows = ctx.enter_context(tc.tile_pool(name="rows", bufs=CHUNKS))
        work = ctx.enter_context(tc.tile_pool(name="work", bufs=3))
        psum_gso = ctx.enter_context(tc.psum_pool(name="psum_gso", bufs=4))
        psum_one = ctx.enter_context(tc.psum_pool(name="psum_one", bufs=1))
        ctx.enter_context(tc.manual_schedule())

        ident = keep.tile([P, P], F32)
        make_identity(nc, ident[:])

        xs = keep.tile([P, CHUNKS, PAIR, K2], BF16)
        x_sb = keep.tile([P, NODES], BF16)
        x2_raw = keep.tile([P, CHUNKS, PAIR, CH], BF16)
        x1_raw = keep.tile([P, CHUNKS, PAIR, CH], BF16)
        w_raw = keep.tile([P, PACK, CH], BF16)
        bias_bf = keep.tile([P, 1], BF16)
        gso_rows = []
        for a in range(CHUNKS):
            gso_chunk = rows.tile([P, PAIR, NODES], BF16, name="gso_chunk")
            gso_rows.append(gso_chunk)

        nc.scalar.dma_start(out=w_raw[0:64, 0:2, :], in_=weight[1].rearrange("(q f) j -> q f j", f=2))
        nc.scalar.dma_start(out=w_raw[0:64, 2:4, :], in_=weight[3].rearrange("(q f) j -> q f j", f=2))
        nc.scalar.dma_start(out=w_raw[64:96, :, :], in_=weight[0].rearrange("(r t) j -> r t j", t=PACK))
        nc.scalar.dma_start(out=w_raw[96:128, :, :], in_=weight[2].rearrange("(r t) j -> r t j", t=PACK))
        nc.scalar.dma_start(out=bias_bf[:], in_=bias.rearrange("(c o) -> c o", o=1))

        def load_x1(n0, n1):
            nc.sync.dma_start(
                out=x1_raw[:, n0:n1].rearrange("p a e c -> p a (e c)"), in_=x1_split[:, n0:n1]
            )

        def load_x(n0, n1):
            nc.sync.dma_start(out=x_sb[:, n0 * CHUNK : n1 * CHUNK], in_=x_cn[:, n0 * CHUNK : n1 * CHUNK])

        def load_x2():
            nc.sync.dma_start(out=x2_raw[:].rearrange("p a e c -> p a (e c)"), in_=x2_split)

        def load_gso(a, es=(0, 1)):
            for e in es:
                nc.sync.dma_start(out=gso_rows[a][:, e, :], in_=gso_split[a, :, e, :])

        load_gso(0)
        load_x2()
        load_gso(1)
        load_x1(0, 4)
        load_x(0, 4)
        for a in range(2, 6):
            load_gso(a)
        load_x1(4, 6)
        load_x(4, 6)
        load_gso(6)
        load_gso(7)
        load_x1(6, 8)
        load_x(6, 8)

        w_grouped = keep.tile([P, CH, PACK], BF16, align_bytes=64)
        w_codes = keep.tile([P, CH], U32, align_bytes=64)
        w_scales = keep.tile([P, CH], U8, align_bytes=64)

        def quantise_weight():
            nc.scalar.copy(out=w_grouped[:], in_=w_raw[:].rearrange("p t j -> p j t"))
            nc.vector.quantize_mx(
                out=w_codes[:].bitcast(FP8X4), scales=w_scales[:], in_=w_grouped[:].rearrange("p j t -> p (j t)")
            )

        x2_grouped = keep.tile([P, PASSES, CH, PACK], BF16, align_bytes=64)
        x2_codes = keep.tile([P, PASSES, CH], U32, align_bytes=64)
        x2_scales = keep.tile([P, PASSES, CH], U8, align_bytes=64)

        def quantise_x2():
            for g in range(PASSES):
                (nc.vector.tensor_copy if g < 2 else nc.scalar.copy)(
                    out=x2_grouped[:, g].rearrange("p c (u e) -> p c u e", e=PAIR),
                    in_=x2_raw[:, 2 * g : 2 * g + 2, :, :].rearrange("p u e c -> p c u e"),
                )
            nc.vector.quantize_mx(
                out=x2_codes[:].rearrange("p g c -> p (g c)").bitcast(FP8X4),
                scales=x2_scales[:].rearrange("p g c -> p (g c)"),
                in_=x2_grouped[:].rearrange("p g c t -> p (g c t)"),
            )

        x_words = x_sb[:].bitcast(F32)
        xs_words = xs[:].bitcast(F32)

        def place_x1(a0, a1):
            nc.vector.tensor_copy(out=xs[:, a0:a1, :, X1_AT : X1_AT + CH], in_=x1_raw[:, a0:a1])

        def place_x2(a0, a1):
            nc.vector.tensor_copy(
                out=xs_words[:, a0:a1].rearrange("p a e (u w) -> p (a e) u w", u=2)[
                    :, :, :, X2_AT // 2 : X2_AT // 2 + CH // PACK
                ],
                in_=x2_raw[:, a0:a1].bitcast(F32).rearrange("p a e (r u) -> p (a e) u r", u=2),
            )

        gso_grouped = {}
        gso_codes = {}
        gso_scales = {}
        x3_acc = {}
        xs_grouped = {}
        xs_codes = {}
        xs_scales = {}
        out_acc = {}
        x3_pair = {}
        LAST = CHUNKS - 1

        def transpose_gso(a, e, copies):
            words = gso_rows[a][:].bitcast(F32)
            grouped = work.tile([P, PASSES, P, PACK], BF16, name="gso_grouped", align_bytes=64, bufs=4)
            grouped_words = grouped[:].bitcast(F32)
            for half in range(PASSES // 2):
                bank = psum_gso.tile([P, 2, 2, P], F32, name="gso_bank")
                for g2 in range(2):
                    for u in range(2):
                        first = (4 * half + 2 * g2 + u) * P
                        nc.tensor.transpose(bank[:, g2, u, :], words[:, e, first : first + P], ident[:])
                copies[half](
                    out=grouped_words[:, 2 * half : 2 * half + 2],
                    in_=bank[:].rearrange("q g u n -> q g n u"),
                )
            gso_grouped[(a, e)] = grouped

        def quantise_gso(a, e, parts=1):
            codes = work.tile([P, PASSES, P], U32, name="gso_codes", align_bytes=64, bufs=6)
            scales = work.tile([P, PASSES, P], U8, name="gso_scales", align_bytes=64, bufs=6)
            for part in range(parts):
                g = slice(part * PASSES // parts, (part + 1) * PASSES // parts)
                nc.vector.quantize_mx(
                    out=codes[:, g].rearrange("q g n -> q (g n)").bitcast(FP8X4),
                    scales=scales[:, g].rearrange("q g n -> q (g n)"),
                    in_=gso_grouped[(a, e)][:, g].rearrange("q g n t -> q (g n t)"),
                )
            gso_codes[(a, e)] = codes
            gso_scales[(a, e)] = scales

        def transpose_x(chunks):
            bank = psum_one.tile([P, len(chunks), CH], F32, name="x_bank")
            for i, a in enumerate(chunks):
                nc.tensor.transpose(bank[:, i], x_words[:, a * P : (a + 1) * P], ident[:])
            for i, a in enumerate(chunks):
                values = bank[:, i].bitcast(BF16).rearrange("p (r u f e) -> p e u r f", u=2, f=2, e=PAIR)
                for e in range(PAIR):
                    halves = xs[:, a, e, :].rearrange("p (u s) -> p u s", u=2)
                    nc.scalar.copy(
                        out=halves[:, :, X0_AT : X0_AT + CH // 2].rearrange("p u (r f) -> p u r f", f=2),
                        in_=values[:, e],
                    )

        def first_matmul(a, e):
            if a == LAST:
                acc = psum_gso.tile([P, 1, CH], F32, name="gso_bank")
                x3_acc[(a, e)] = acc[:]
            else:
                if e == 0:
                    x3_pair[a] = psum_one.tile([P, PAIR, CH], F32, name="x3_acc")
                acc = x3_pair[a]
                x3_acc[(a, e)] = acc[:, e : e + 1]
            for g in range(PASSES):
                nc.tensor.matmul_mx(
                    out=x3_acc[(a, e)][:, 0],
                    lhsT=gso_codes[(a, e)][:, g, :].bitcast(FP8X4),
                    lhsT_scale=gso_scales[(a, e)][:, g, :],
                    rhs=x2_codes[:, g, :].bitcast(FP8X4),
                    rhs_scale=x2_scales[:, g, :],
                    start=(g == 0),
                    stop=(g == PASSES - 1),
                )

        def finish_x3(a, es=(0, 1)):
            nc.vector.scalar_tensor_tensor(
                out=xs[:, a, es[0] : es[-1] + 1, X3_AT : X3_AT + CH],
                in0=x3_pair[a][:] if a < LAST else x3_acc[(a, es[0])],
                scalar=2.0,
                in1=x1_raw[:, a, es[0] : es[-1] + 1],
                op0=MULT,
                op1=SUBTRACT,
            )

        def transpose_xs(a, es=(0, 1)):
            if a < LAST:
                bank = psum_one.tile([P, len(es), 2, P], F32, name="xs_bank")
            else:
                bank = psum_gso.tile([P, len(es), 2, P], F32, name="gso_bank")
            for i, e in enumerate(es):
                for u in range(2):
                    nc.tensor.transpose(bank[:, i, u, :], xs_words[:, a, e, u * P : (u + 1) * P], ident[:])
            grouped = work.tile([P, len(es), P, PACK], BF16, name="xs_grouped", align_bytes=64, bufs=5)
            nc.scalar.copy(
                out=grouped[:].bitcast(F32),
                in_=bank[:].rearrange("q e u p -> q e p u"),
            )
            xs_grouped[(a, es)] = grouped

        def quantise_xs(a, es=(0, 1)):
            codes = work.tile([P, len(es) * P], U32, name="xs_codes", align_bytes=64, bufs=5)
            scales = work.tile([P, len(es) * P], U8, name="xs_scales", align_bytes=64, bufs=5)
            nc.vector.quantize_mx(
                out=codes[:].bitcast(FP8X4), scales=scales[:], in_=xs_grouped[(a, es)][:].rearrange("q e p t -> q (e p t)")
            )
            xs_codes[(a, es)] = codes
            xs_scales[(a, es)] = scales

        def second_matmul(a, es=(0, 1)):
            if a < LAST:
                out_acc[a] = psum_one.tile([P, PAIR, P], F32, name="out_acc")
            elif 0 in es:
                out_acc[a] = psum_gso.tile([P, PAIR, P], F32, name="gso_bank")
            nc.tensor.matmul_mx(
                out=out_acc[a][:, es[0] : es[-1] + 1, :].rearrange("j e p -> j (e p)"),
                lhsT=w_codes[:].bitcast(FP8X4),
                lhsT_scale=w_scales[:],
                rhs=xs_codes[(a, es)][:].bitcast(FP8X4),
                rhs_scale=xs_scales[(a, es)][:],
                start=True,
                stop=True,
            )

        def finish_out(a):
            nodes = slice(a * CHUNK, (a + 1) * CHUNK)
            result = work.tile([P, P, PAIR], F32, name="result", bufs=4)
            nc.vector.scalar_tensor_tensor(
                out=result[:],
                in0=out_acc[a][:].rearrange("j e p -> j p e"),
                scalar=bias_bf[:, 0:1],
                in1=x_sb[:, nodes].rearrange("j (p e) -> j p e", e=PAIR),
                op0=ADD,
                op1=ADD,
            )
            nc.sync.dma_start(out=out_cn[:, nodes], in_=result[:].rearrange("j p e -> j (p e)"))

        S, V = nc.scalar.copy, nc.vector.tensor_copy

        transpose_gso(0, 0, (S, V))
        transpose_gso(0, 1, (S, V))
        quantise_x2()
        quantise_weight()
        for i in range(1, CHUNKS):
            quantise_gso(i - 1, 0)
            if i == 6:
                place_x1(4, 6)
                transpose_x(range(4, 6))
            if i >= 2:
                finish_x3(i - 2)
            if i >= 4:
                finish_out(i - 4)
            quantise_gso(i - 1, 1)
            if i >= 3:
                quantise_xs(i - 3)
            transpose_gso(i, 0, (S, S))
            transpose_gso(i, 1, (S, V if i % 2 == 1 and i < LAST else S))
            if i >= 2:
                transpose_xs(i - 2)
            first_matmul(i - 1, 0)
            first_matmul(i - 1, 1)
            if i >= 3:
                second_matmul(i - 3)
            if i == 1:
                place_x2(0, CHUNKS)
                place_x1(0, 4)
                transpose_x(range(4))
        quantise_gso(7, 0)
        transpose_x(range(6, 8))
        first_matmul(7, 0)
        place_x1(6, 8)
        quantise_gso(7, 1, 2)
        finish_x3(6)
        first_matmul(7, 1)
        transpose_xs(6)
        finish_x3(7, (0,))
        quantise_xs(5)
        transpose_xs(7, (0,))
        finish_x3(7, (1,))
        finish_out(4)
        transpose_xs(7, (1,))
        second_matmul(5)
        quantise_xs(6)
        finish_out(5)
        second_matmul(6)
        quantise_xs(7, (0,))
        second_matmul(7, (0,))
        quantise_xs(7, (1,))
        second_matmul(7, (1,))
        finish_out(6)
        finish_out(7)
